import numpy as np
import ml_dtypes


def mxq(x, axis, fmt="e4m3"):
    dtype, down = {"e4m3": (ml_dtypes.float8_e4m3fn, 7), "e5m2": (ml_dtypes.float8_e5m2, 14)}[fmt]
    v = np.moveaxis(np.asarray(x, np.float32).astype(ml_dtypes.bfloat16).astype(np.float64), axis, -1)
    blocks = v.reshape(v.shape[:-1] + (-1, 32))
    amax = np.abs(blocks).max(-1, keepdims=True)
    byte = np.maximum(np.where(amax > 0, np.frexp(amax)[1] - 1 + 127, 0) - down, 1)
    scale = np.exp2(byte - 127.0)
    codes = (blocks / scale).astype(np.float32).astype(dtype).astype(np.float64)
    return np.moveaxis((codes * scale).reshape(v.shape), -1, axis)


WIDE = False


def mx_kscale(k):
    if not WIDE:
        return np.ones(k)
    levels = np.array([10, -10, 5, -5, 0])
    a = np.random.permutation(np.resize(levels, k // 512 * 4)).reshape(k // 512, 4)
    idx = np.arange(k)
    return np.exp2(a[idx // 512, idx % 128 // 32])


BF16 = ml_dtypes.bfloat16


def bf(x):
    return np.asarray(x, np.float32).astype(BF16)


def f64(x):
    return np.asarray(x).astype(np.float64)


B, CH, CQ, CV, H, W = 1, 1024, 128, 512, 32, 64
EPS = 1e-5
POOL = 2
HW = H * W
HW4 = HW // (POOL * POOL)
A = 1.7 / CQ ** 0.25


def vec(c, z):
    return bf(z * np.random.standard_normal(c))


def pos(c):
    return bf(0.5 + np.random.random(c))


def setup_inputs():
    t = mx_kscale(CV)
    return {'q': bf(A * np.random.standard_normal((B, HW, CQ))),
            'k': bf(A * (1.0 + 0.7 * np.random.standard_normal((B, CQ, HW4)))),
            'v': bf((1.0 + 0.7 * np.random.standard_normal((B, HW4, CV))) * t),
            'x': bf(np.random.standard_normal((B, CH, H, W))),
            'wp': bf(np.random.standard_normal((CH, CV)) / np.sqrt(CV) / t), 'bp': vec(CH, 0.2),
            'bnp_s': pos(CH), 'bnp_b': vec(CH, 0.2), 'bnp_m': vec(CH, 0.2), 'bnp_v': pos(CH),
            'gamma': bf(0.7 + 0.1 * np.random.standard_normal(1))}


def reference(q, k, v, x, wp, bp, bnp_s, bnp_b, bnp_m, bnp_v, gamma):
    s = f64(q) @ f64(k)
    e = np.exp(s - s.max(-1, keepdims=True))
    g = (mxq(e, 2, 'e4m3') @ mxq(f64(v), 1, 'e4m3')) / e.sum(-1, keepdims=True)
    gt = g.transpose(0, 2, 1)
    y = (mxq(f64(wp), 1, 'e4m3') @ mxq(gt, 1, 'e4m3')) + f64(bp)[None, :, None]
    inv = f64(bnp_s) / np.sqrt(f64(bnp_v) + EPS)
    z = y * inv[None, :, None] + (f64(bnp_b) - f64(bnp_m) * inv)[None, :, None]
    return f64(x) + f64(gamma) * z.reshape(B, CH, H, W)

@@ -1,0 +1,393 @@
+from contextlib import ExitStack
+
+import concourse.mybir as mybir
+from concourse.masks import make_identity
+
+F32 = mybir.dt.float32
+BF16 = mybir.dt.bfloat16
+U32 = mybir.dt.uint32
+U8 = mybir.dt.uint8
+FP8X4 = mybir.dt.float8_e4m3fn_x4
+ALU = mybir.AluOpType
+ACT = mybir.ActivationFunctionType
+AXIS = mybir.AxisListType
+
+P = 128
+PACK = 4
+POSITIONS = 2048
+QUERY_CH = 128
+POOLED = 512
+VALUE_CH = 512
+OUT_CH = 1024
+EPS = 1e-5
+
+TILES = POSITIONS // P
+GROUP = 4
+GROUP_POS = GROUP * P
+GROUPS = TILES // GROUP
+BLOCKS = OUT_CH // P
+PIECES = GROUPS * BLOCKS // 2
+PIECES_PER_GROUP = BLOCKS // 2
+
+FLOPS = 2 * POSITIONS * POOLED * (QUERY_CH + VALUE_CH) + 2 * OUT_CH * VALUE_CH * POSITIONS
+
+
+def tile_selfattention_pb_kernel(
+    tc, q, k, v, x, wp, bp, bnp_s, bnp_b, bnp_m, bnp_v, gamma, out
+):
+    nc = tc.nc
+    with ExitStack() as ctx:
+        const = ctx.enter_context(tc.tile_pool(name="const", bufs=1))
+        work = ctx.enter_context(tc.tile_pool(name="work", bufs=3))
+        psum = ctx.enter_context(tc.psum_pool(name="psum", bufs=1))
+
+        q_view = q.rearrange("b (i p) c -> p (b i) c", p=P)
+        x_view = x.rearrange("b (cb p) h w -> p (b cb) (h w)", p=P)
+        out_view = out.rearrange("b (cb p) h w -> p (b cb) (h w)", p=P)
+
+        q_raw = []
+        x_sb = []
+        for g in range(GROUPS):
+            q_raw.append(const.tile([P, GROUP, QUERY_CH], BF16, name="q_raw%d" % g))
+            x_sb.append(const.tile([P, BLOCKS, GROUP_POS], BF16, name="x_sb%d" % g))
+        k_raw = const.tile([P, POOLED], BF16)
+        v_raw = const.tile([P, PACK, VALUE_CH], BF16)
+        wp_raw = const.tile([P, BLOCKS, VALUE_CH], BF16)
+        vec_rows = const.tile([P, P], BF16)
+        gamma_bf = const.tile([P, 1], BF16)
+
+        def load_q(g):
+            nc.sync.dma_start(out=q_raw[g][:], in_=q_view[:, g * GROUP : (g + 1) * GROUP, :])
+
+        def load_x(g):
+            nc.sync.dma_start(
+                out=x_sb[g][:], in_=x_view[:, :, g * GROUP_POS : (g + 1) * GROUP_POS]
+            )
+
+        load_q(0)
+        nc.sync.dma_start(out=k_raw[:], in_=k.rearrange("b c n -> (b c) n"))
+        nc.sync.dma_start(out=v_raw[:], in_=v.rearrange("b (p j) c -> p (b j) c", j=PACK))
+        load_q(1)
+        nc.sync.dma_start(out=wp_raw[:], in_=wp.rearrange("(cb p) c -> p cb c", p=P))
+
+        nc.vector.memset(vec_rows[:], 0.0)
+        for j, vec in enumerate((bp, bnp_s, bnp_b, bnp_m, bnp_v)):
+            nc.scalar.dma_start(
+                out=vec_rows[j * BLOCKS : (j + 1) * BLOCKS, :],
+                in_=vec.rearrange("(cb p) -> cb p", p=P),
+            )
+        nc.scalar.dma_start(out=gamma_bf[:], in_=gamma.partition_broadcast(P))
+
+        load_x(0)
+        load_q(2)
+        load_q(3)
+        for g in range(1, GROUPS):
+            load_x(g)
+
+        ident_bf = const.tile([P, P], BF16)
+        make_identity(nc, ident_bf[:])
+        ident_f32 = const.tile([P, P], F32)
+        make_identity(nc, ident_f32[:])
+        neg_half = const.tile([P, BLOCKS], F32)
+        nc.gpsimd.memset(neg_half[:], -0.5)
+
+        warm_in = const.tile([P, 1], F32)
+        warm_out = const.tile([P, 1], F32)
+        nc.vector.memset(warm_in[:], 0.0)
+        nc.scalar.activation(out=warm_out[:], in_=warm_in[:], func=ACT.Exp)
+
+        k_perm = const.tile([P, PACK, P], BF16)
+        nc.vector.tensor_copy(out=k_perm[:], in_=k_raw[:].rearrange("c (p t) -> c t p", t=PACK))
+
+        neg_max = const.tile([P, TILES], F32)
+        row_sum = const.tile([P, TILES], F32)
+        inv_sum = const.tile([P, TILES], F32)
+
+        qT = []
+        for g in range(GROUPS):
+            qT.append(const.tile([P, GROUP, P], BF16, name="qT%d" % g))
+
+        v_grouped = const.tile([P, VALUE_CH, PACK], BF16, align_bytes=64)
+        v_codes = const.tile([P, VALUE_CH], U32, align_bytes=64)
+        v_scales = const.tile([P, VALUE_CH], U8, align_bytes=64)
+        wp_grouped = const.tile([P, OUT_CH, PACK], BF16, align_bytes=64)
+        wp_codes = const.tile([P, OUT_CH], U32, align_bytes=64)
+        wp_scales = const.tile([P, OUT_CH], U8, align_bytes=64)
+
+        vec_cols = const.tile([P, 5 * BLOCKS], F32)
+        gamma_f32 = const.tile([P, 1], F32)
+        var_eps = const.tile([P, BLOCKS], F32)
+        rstd = const.tile([P, BLOCKS], F32)
+        inv = const.tile([P, BLOCKS], F32)
+        centred = const.tile([P, BLOCKS], F32)
+        scaled = const.tile([P, BLOCKS], F32)
+        shifted = const.tile([P, BLOCKS], F32)
+        gain = const.tile([P, BLOCKS], F32)
+        shift = const.tile([P, BLOCKS], F32)
+
+        s_ps = {}
+        e_bf = {}
+        e_codes = {}
+        e_scales = {}
+        r_sb = {}
+        g_grouped = {}
+        g_codes = {}
+        g_scales = {}
+        y_ps = {}
+        o_sb = {}
+
+        def transpose_q(g):
+            qT_ps = psum.tile([P, GROUP, P], BF16, tag="tp")
+            for il in range(GROUP):
+                nc.tensor.transpose(qT_ps[:, il, :], q_raw[g][:, il, :], ident_bf[:])
+            nc.scalar.copy(out=qT[g][:], in_=qT_ps[:])
+
+        def scores(i):
+            g, il = divmod(i, GROUP)
+            s_ps[i] = psum.tile([P, POOLED], F32, tag="s", bufs=2, name="s_ps")
+            nc.tensor.matmul(
+                s_ps[i][:],
+                lhsT=qT[g][:, il, :],
+                rhs=k_perm[:].rearrange("c t p -> c (t p)"),
+                start=True,
+                stop=True,
+            )
+
+        def softmax_numerator(i):
+            nc.vector.tensor_reduce(
+                out=neg_max[:, i : i + 1], in_=s_ps[i][:], axis=AXIS.X, op=ALU.max, negate=True
+            )
+            e_bf[i] = work.tile([P, PACK, P], BF16, tag="e_bf", name="e_bf")
+            nc.scalar.activation(
+                out=e_bf[i][:].rearrange("r t p -> r (t p)"),
+                in_=s_ps[i][:],
+                func=ACT.Exp,
+                bias=neg_max[:, i : i + 1],
+                scale=1.0,
+                accum_out=row_sum[:, i : i + 1],
+            )
+
+        def reciprocal_of_sum(i):
+            nc.vector.reciprocal(out=inv_sum[:, i : i + 1], in_=row_sum[:, i : i + 1])
+
+        def transpose_e(i):
+            eT_ps = psum.tile([P, PACK, P], BF16, tag="tp")
+            for t in range(PACK):
+                nc.tensor.transpose(eT_ps[:, t, :], e_bf[i][:, t, :], ident_bf[:])
+            r_ps = psum.tile([P, P], F32, tag="r")
+            nc.tensor.transpose(r_ps[:], inv_sum[:, i : i + 1].to_broadcast([P, P]), ident_f32[:])
+            e_grouped = work.tile([P, P, PACK], BF16, tag="e_grouped", align_bytes=64)
+            nc.scalar.copy(out=e_grouped[:], in_=eT_ps[:].rearrange("p t r -> p r t"))
+            r_sb[i] = work.tile([P, P], F32, tag="r_sb", name="r_sb")
+            nc.scalar.copy(out=r_sb[i][:], in_=r_ps[:])
+            return e_grouped
+
+        def quantise_e(i, e_grouped):
+            e_codes[i] = work.tile([P, P], U32, tag="e_codes", name="e_codes", align_bytes=64)
+            e_scales[i] = work.tile([P, P], U8, tag="e_scales", name="e_scales", align_bytes=64)
+            nc.vector.quantize_mx(
+                out=e_codes[i][:].bitcast(FP8X4),
+                scales=e_scales[i][:],
+                in_=e_grouped[:].rearrange("p r t -> p (r t)"),
+            )
+
+        def attend(i):
+            g_ps = psum.tile([P, PACK, P], F32, tag="g", bufs=2)
+            for t in range(PACK):
+                cols = slice(t * P, (t + 1) * P)
+                nc.tensor.matmul_mx(
+                    out=g_ps[:, t, :],
+                    lhsT=v_codes[:, cols].bitcast(FP8X4),
+                    lhsT_scale=v_scales[:, cols],
+                    rhs=e_codes[i][:].bitcast(FP8X4),
+                    rhs_scale=e_scales[i][:],
+                    start=True,
+                    stop=True,
+                )
+            return g_ps
+
+        def normalise(i, g_ps):
+            g_grouped[i] = work.tile(
+                [P, P, PACK], BF16, tag="g_grouped", name="g_grouped", align_bytes=64
+            )
+            nc.vector.tensor_tensor(
+                out=g_grouped[i][:],
+                in0=g_ps[:].rearrange("p t r -> p r t"),
+                in1=r_sb[i][:].unsqueeze(2).to_broadcast([P, P, PACK]),
+                op=ALU.mult,
+            )
+
+        def quantise_g(i):
+            g, il = divmod(i, GROUP)
+            if il == 0:
+                g_codes[g] = work.tile(
+                    [P, GROUP_POS], U32, tag="g_codes", name="g_codes", align_bytes=64
+                )
+                g_scales[g] = work.tile(
+                    [P, GROUP_POS], U8, tag="g_scales", name="g_scales", align_bytes=64
+                )
+            cols = slice(il * P, (il + 1) * P)
+            nc.vector.quantize_mx(
+                out=g_codes[g][:, cols].bitcast(FP8X4),
+                scales=g_scales[g][:, cols],
+                in_=g_grouped[i][:].rearrange("p r t -> p (r t)"),
+            )
+
+        def blocks_of(piece):
+            g, half = divmod(piece, PIECES_PER_GROUP)
+            return g, 2 * half, 2 * half + 1
+
+        def add_shift_to_x(piece):
+            g, cb, cb_scalar = blocks_of(piece)
+            o_sb[(g, cb)] = work.tile([P, GROUP_POS], F32, tag="o_vector", bufs=6, name="o_vector")
+            nc.gpsimd.tensor_scalar(
+                out=o_sb[(g, cb)][:],
+                in0=x_sb[g][:, cb, :],
+                scalar1=1.0,
+                scalar2=shift[:, cb : cb + 1],
+                op0=ALU.mult,
+                op1=ALU.add,
+            )
+
+        def project(piece):
+            g, cb_a, cb_b = blocks_of(piece)
+            for cb in (cb_a, cb_b):
+                cols = slice(cb * P, (cb + 1) * P)
+                y_ps[(g, cb)] = psum.tile([P, GROUP_POS], F32, tag="y", bufs=2, name="y_ps")
+                nc.tensor.matmul_mx(
+                    out=y_ps[(g, cb)][:],
+                    lhsT=wp_codes[:, cols].bitcast(FP8X4),
+                    lhsT_scale=wp_scales[:, cols],
+                    rhs=g_codes[g][:].bitcast(FP8X4),
+                    rhs_scale=g_scales[g][:],
+                    start=True,
+                    stop=True,
+                )
+
+        def finish(piece):
+            g, cb_v, cb_s = blocks_of(piece)
+            pos = slice(g * GROUP_POS, (g + 1) * GROUP_POS)
+            nc.vector.scalar_tensor_tensor(
+                out=o_sb[(g, cb_v)][:],
+                in0=y_ps[(g, cb_v)][:],
+                scalar=gain[:, cb_v : cb_v + 1],
+                in1=o_sb[(g, cb_v)][:],
+                op0=ALU.mult,
+                op1=ALU.add,
+            )
+            nc.sync.dma_start(out=out_view[:, cb_v, pos], in_=o_sb[(g, cb_v)][:])
+            o_scalar = work.tile([P, GROUP_POS], F32, tag="o_scalar", bufs=4)
+            nc.scalar.activation(
+                out=o_scalar[:],
+                in_=y_ps[(g, cb_s)][:],
+                func=ACT.Identity,
+                bias=shift[:, cb_s : cb_s + 1],
+                scale=gain[:, cb_s : cb_s + 1],
+            )
+            nc.gpsimd.tensor_tensor(
+                out=o_scalar[:], in0=o_scalar[:], in1=x_sb[g][:, cb_s, :], op=ALU.add
+            )
+            nc.sync.dma_start(out=out_view[:, cb_s, pos], in_=o_scalar[:])
+
+        def regroup_v():
+            nc.vector.tensor_copy(
+                out=v_grouped[:].rearrange("p (t m) j -> p t m j", t=PACK),
+                in_=v_raw[:].rearrange("p j (m t) -> p t m j", t=PACK),
+            )
+
+        def quantise_v():
+            nc.vector.quantize_mx(
+                out=v_codes[:].bitcast(FP8X4),
+                scales=v_scales[:],
+                in_=v_grouped[:].rearrange("p c j -> p (c j)"),
+            )
+
+        wp_words = wp_raw[:].bitcast(F32).rearrange("r b (p u) -> r b u p", u=2)
+        wp_grouped_words = wp_grouped[:].bitcast(F32)
+
+        def transpose_wp(pair):
+            wT_ps = psum.tile([P, 2, 2, P], F32, tag="y", bufs=2)
+            for c in range(2):
+                for u in range(2):
+                    nc.tensor.transpose(
+                        wT_ps[:, c, u, :], wp_words[:, 2 * pair + c, u, :], ident_f32[:]
+                    )
+            nc.vector.tensor_copy(
+                out=wp_grouped_words[:, 2 * pair * P : (2 * pair + 2) * P, :].rearrange(
+                    "p (c r) u -> p c r u", c=2
+                ),
+                in_=wT_ps[:].rearrange("p c u r -> p c r u"),
+            )
+
+        def quantise_wp(half):
+            rows = slice(half * OUT_CH // 2, (half + 1) * OUT_CH // 2)
+            nc.vector.quantize_mx(
+                out=wp_codes[:, rows].bitcast(FP8X4),
+                scales=wp_scales[:, rows],
+                in_=wp_grouped[:, rows, :].rearrange("p r t -> p (r t)"),
+            )
+
+        def channel_constants_first():
+            vec_ps = psum.tile([P, P], BF16, tag="r")
+            nc.tensor.transpose(vec_ps[:], vec_rows[:], ident_bf[:])
+            nc.vector.tensor_copy(out=vec_cols[:], in_=vec_ps[:, 0 : 5 * BLOCKS])
+            nc.vector.tensor_copy(out=gamma_f32[:], in_=gamma_bf[:])
+            nc.vector.tensor_scalar_add(
+                out=var_eps[:], in0=vec_cols[:, 4 * BLOCKS : 5 * BLOCKS], scalar1=EPS
+            )
+            nc.gpsimd.tensor_tensor(out=rstd[:], in0=var_eps[:], in1=neg_half[:], op=ALU.pow)
+
+        def channel_constants_second():
+            bias_c = vec_cols[:, 0:BLOCKS]
+            gain_c = vec_cols[:, BLOCKS : 2 * BLOCKS]
+            beta_c = vec_cols[:, 2 * BLOCKS : 3 * BLOCKS]
+            mean_c = vec_cols[:, 3 * BLOCKS : 4 * BLOCKS]
+            nc.vector.tensor_tensor(out=centred[:], in0=bias_c, in1=mean_c, op=ALU.subtract)
+            nc.vector.tensor_tensor(out=inv[:], in0=gain_c, in1=rstd[:], op=ALU.mult)
+            nc.vector.tensor_scalar_mul(out=gain[:], in0=inv[:], scalar1=gamma_f32[:, 0:1])
+            nc.vector.tensor_tensor(out=scaled[:], in0=centred[:], in1=inv[:], op=ALU.mult)
+            nc.vector.tensor_tensor(out=shifted[:], in0=scaled[:], in1=beta_c, op=ALU.add)
+            nc.vector.tensor_scalar_mul(out=shift[:], in0=shifted[:], scalar1=gamma_f32[:, 0:1])
+
+        PROJECT_LAG = GROUP + 1
+        transpose_q(0)
+        scores(0)
+        for n in range(PIECES + PROJECT_LAG + 1):
+            if 1 <= n <= TILES:
+                reciprocal_of_sum(n - 1)
+            if n + 1 < TILES:
+                scores(n + 1)
+            if n < TILES:
+                softmax_numerator(n)
+            if n == 0:
+                regroup_v()
+            if n == 3:
+                channel_constants_second()
+            if 1 <= n <= TILES:
+                e_grouped = transpose_e(n - 1)
+            if n % GROUP == 1 and n // GROUP + 1 < GROUPS:
+                transpose_q(n // GROUP + 1)
+            if n == 2:
+                channel_constants_first()
+            if 2 <= n < 2 + BLOCKS // 2:
+                transpose_wp(n - 2)
+            if 2 <= n < TILES + 2:
+                g_ps = attend(n - 2)
+            if 0 <= n - PROJECT_LAG - 1 < PIECES:
+                finish(n - PROJECT_LAG - 1)
+            if 2 <= n < TILES + 2:
+                normalise(n - 2, g_ps)
+            if n == 1:
+                quantise_v()
+            if 1 <= n <= TILES:
+                quantise_e(n - 1, e_grouped)
+            if 2 <= n < TILES + 2:
+                quantise_g(n - 2)
+            if n == 4:
+                quantise_wp(0)
+            if n == 6:
+                quantise_wp(1)
+            if 0 <= n - PROJECT_LAG < PIECES:
+                project(n - PROJECT_LAG)
+            if 0 <= n - PROJECT_LAG + 2 < PIECES:
+                add_shift_to_x(n - PROJECT_LAG + 2)

@@ -26,8 +26,8 @@ GROUP = 4
 GROUP_POS = GROUP * P
 GROUPS = TILES // GROUP
 BLOCKS = OUT_CH // P
-PIECES = GROUPS * BLOCKS // 2
-PIECES_PER_GROUP = BLOCKS // 2
+PAIRS = BLOCKS // 2
+PIECES = GROUPS * PAIRS
 
 FLOPS = 2 * POSITIONS * POOLED * (QUERY_CH + VALUE_CH) + 2 * OUT_CH * VALUE_CH * POSITIONS
 
@@ -37,19 +37,22 @@ def tile_selfattention_pb_kernel(
 ):
     nc = tc.nc
     with ExitStack() as ctx:
+        ctx.enter_context(tc.manual_schedule())
         const = ctx.enter_context(tc.tile_pool(name="const", bufs=1))
         work = ctx.enter_context(tc.tile_pool(name="work", bufs=3))
         psum = ctx.enter_context(tc.psum_pool(name="psum", bufs=1))
 
         q_view = q.rearrange("b (i p) c -> p (b i) c", p=P)
-        x_view = x.rearrange("b (cb p) h w -> p (b cb) (h w)", p=P)
-        out_view = out.rearrange("b (cb p) h w -> p (b cb) (h w)", p=P)
+        x_view = x.rearrange("b (pair two p) h w -> p two (b pair) (h w)", two=2, p=P)
+        out_view = out.rearrange("b (pair two p) h w -> p two (b pair) (h w)", two=2, p=P)
 
         q_raw = []
-        x_sb = []
+        x_even = []
+        x_odd = []
         for g in range(GROUPS):
             q_raw.append(const.tile([P, GROUP, QUERY_CH], BF16, name="q_raw%d" % g))
-            x_sb.append(const.tile([P, BLOCKS, GROUP_POS], BF16, name="x_sb%d" % g))
+            x_even.append(const.tile([P, PAIRS, GROUP_POS], BF16, name="x_even%d" % g))
+            x_odd.append(const.tile([P, PAIRS, GROUP_POS], BF16, name="x_odd%d" % g))
         k_raw = const.tile([P, POOLED], BF16)
         v_raw = const.tile([P, PACK, VALUE_CH], BF16)
         wp_raw = const.tile([P, BLOCKS, VALUE_CH], BF16)
@@ -59,15 +62,14 @@ def tile_selfattention_pb_kernel(
         def load_q(g):
             nc.sync.dma_start(out=q_raw[g][:], in_=q_view[:, g * GROUP : (g + 1) * GROUP, :])
 
-        def load_x(g):
+        def load_x(tiles, parity, g):
             nc.sync.dma_start(
-                out=x_sb[g][:], in_=x_view[:, :, g * GROUP_POS : (g + 1) * GROUP_POS]
+                out=tiles[g][:], in_=x_view[:, parity, :, g * GROUP_POS : (g + 1) * GROUP_POS]
             )
 
         load_q(0)
         nc.sync.dma_start(out=k_raw[:], in_=k.rearrange("b c n -> (b c) n"))
         nc.sync.dma_start(out=v_raw[:], in_=v.rearrange("b (p j) c -> p (b j) c", j=PACK))
-        load_q(1)
         nc.sync.dma_start(out=wp_raw[:], in_=wp.rearrange("(cb p) c -> p cb c", p=P))
 
         nc.vector.memset(vec_rows[:], 0.0)
@@ -78,11 +80,14 @@ def tile_selfattention_pb_kernel(
             )
         nc.scalar.dma_start(out=gamma_bf[:], in_=gamma.partition_broadcast(P))
 
-        load_x(0)
-        load_q(2)
-        load_q(3)
         for g in range(1, GROUPS):
-            load_x(g)
+            load_q(g)
+        load_x(x_even, 0, 0)
+        load_x(x_even, 0, 1)
+        for g in range(GROUPS):
+            load_x(x_odd, 1, g)
+            if g + 2 < GROUPS:
+                load_x(x_even, 0, g + 2)
 
         ident_bf = const.tile([P, P], BF16)
         make_identity(nc, ident_bf[:])
@@ -125,22 +130,30 @@ def tile_selfattention_pb_kernel(
         gain = const.tile([P, BLOCKS], F32)
         shift = const.tile([P, BLOCKS], F32)
 
+        nc.gpsimd.tensor_scalar(
+            out=v_grouped[:].rearrange("p (t m) j -> p t m j", t=PACK),
+            in0=v_raw[:].rearrange("p j (m t) -> p t m j", t=PACK),
+            scalar1=1.0,
+            scalar2=0.0,
+            op0=ALU.mult,
+            op1=ALU.add,
+        )
+
         s_ps = {}
         e_bf = {}
+        eT_ps = {}
+        e_grouped = {}
         e_codes = {}
         e_scales = {}
+        r_ps = {}
         r_sb = {}
+        g_ps = {}
         g_grouped = {}
         g_codes = {}
         g_scales = {}
         y_ps = {}
-        o_sb = {}
-
-        def transpose_q(g):
-            qT_ps = psum.tile([P, GROUP, P], BF16, tag="tp")
-            for il in range(GROUP):
-                nc.tensor.transpose(qT_ps[:, il, :], q_raw[g][:, il, :], ident_bf[:])
-            nc.scalar.copy(out=qT[g][:], in_=qT_ps[:])
+        o_vector = {}
+        waiting = []
 
         def scores(i):
             g, il = divmod(i, GROUP)
@@ -153,10 +166,12 @@ def tile_selfattention_pb_kernel(
                 stop=True,
             )
 
-        def softmax_numerator(i):
+        def row_maximum(i):
             nc.vector.tensor_reduce(
                 out=neg_max[:, i : i + 1], in_=s_ps[i][:], axis=AXIS.X, op=ALU.max, negate=True
             )
+
+        def exponentials(i):
             e_bf[i] = work.tile([P, PACK, P], BF16, tag="e_bf", name="e_bf")
             nc.scalar.activation(
                 out=e_bf[i][:].rearrange("r t p -> r (t p)"),
@@ -171,32 +186,41 @@ def tile_selfattention_pb_kernel(
             nc.vector.reciprocal(out=inv_sum[:, i : i + 1], in_=row_sum[:, i : i + 1])
 
         def transpose_e(i):
-            eT_ps = psum.tile([P, PACK, P], BF16, tag="tp")
+            eT_ps[i] = psum.tile([P, PACK, P], BF16, tag="tp", name="eT_ps")
             for t in range(PACK):
-                nc.tensor.transpose(eT_ps[:, t, :], e_bf[i][:, t, :], ident_bf[:])
-            r_ps = psum.tile([P, P], F32, tag="r")
-            nc.tensor.transpose(r_ps[:], inv_sum[:, i : i + 1].to_broadcast([P, P]), ident_f32[:])
-            e_grouped = work.tile([P, P, PACK], BF16, tag="e_grouped", align_bytes=64)
-            nc.scalar.copy(out=e_grouped[:], in_=eT_ps[:].rearrange("p t r -> p r t"))
-            r_sb[i] = work.tile([P, P], F32, tag="r_sb", name="r_sb")
-            nc.scalar.copy(out=r_sb[i][:], in_=r_ps[:])
-            return e_grouped
+                nc.tensor.transpose(eT_ps[i][:, t, :], e_bf[i][:, t, :], ident_bf[:])
 
-        def quantise_e(i, e_grouped):
+        def copy_e(i):
+            e_grouped[i] = work.tile(
+                [P, P, PACK], BF16, tag="e_grouped", name="e_grouped", align_bytes=64
+            )
+            nc.scalar.copy(out=e_grouped[i][:], in_=eT_ps[i][:].rearrange("p t r -> p r t"))
+
+        def spread_reciprocals(i):
+            r_ps[i] = psum.tile([P, P], F32, tag="r", name="r_ps")
+            nc.tensor.transpose(
+                r_ps[i][:], inv_sum[:, i : i + 1].to_broadcast([P, P]), ident_f32[:]
+            )
+
+        def copy_reciprocals(i):
+            r_sb[i] = work.tile([P, P], F32, tag="r_sb", name="r_sb")
+            nc.scalar.copy(out=r_sb[i][:], in_=r_ps[i][:])
+
+        def quantise_e(i):
             e_codes[i] = work.tile([P, P], U32, tag="e_codes", name="e_codes", align_bytes=64)
             e_scales[i] = work.tile([P, P], U8, tag="e_scales", name="e_scales", align_bytes=64)
             nc.vector.quantize_mx(
                 out=e_codes[i][:].bitcast(FP8X4),
                 scales=e_scales[i][:],
-                in_=e_grouped[:].rearrange("p r t -> p (r t)"),
+                in_=e_grouped[i][:].rearrange("p r t -> p (r t)"),
             )
 
         def attend(i):
-            g_ps = psum.tile([P, PACK, P], F32, tag="g", bufs=2)
+            g_ps[i] = psum.tile([P, PACK, P], F32, tag="g", bufs=2, name="g_ps")
             for t in range(PACK):
                 cols = slice(t * P, (t + 1) * P)
                 nc.tensor.matmul_mx(
-                    out=g_ps[:, t, :],
+                    out=g_ps[i][:, t, :],
                     lhsT=v_codes[:, cols].bitcast(FP8X4),
                     lhsT_scale=v_scales[:, cols],
                     rhs=e_codes[i][:].bitcast(FP8X4),
@@ -204,15 +228,14 @@ def tile_selfattention_pb_kernel(
                     start=True,
                     stop=True,
                 )
-            return g_ps
 
-        def normalise(i, g_ps):
+        def normalise(i):
             g_grouped[i] = work.tile(
                 [P, P, PACK], BF16, tag="g_grouped", name="g_grouped", align_bytes=64
             )
             nc.vector.tensor_tensor(
                 out=g_grouped[i][:],
-                in0=g_ps[:].rearrange("p t r -> p r t"),
+                in0=g_ps[i][:].rearrange("p t r -> p r t"),
                 in1=r_sb[i][:].unsqueeze(2).to_broadcast([P, P, PACK]),
                 op=ALU.mult,
             )
@@ -233,29 +256,30 @@ def tile_selfattention_pb_kernel(
                 in_=g_grouped[i][:].rearrange("p r t -> p (r t)"),
             )
 
-        def blocks_of(piece):
-            g, half = divmod(piece, PIECES_PER_GROUP)
-            return g, 2 * half, 2 * half + 1
-
         def add_shift_to_x(piece):
-            g, cb, cb_scalar = blocks_of(piece)
-            o_sb[(g, cb)] = work.tile([P, GROUP_POS], F32, tag="o_vector", bufs=6, name="o_vector")
+            g, pair = divmod(piece, PAIRS)
+            o_vector[piece] = work.tile(
+                [P, GROUP_POS], F32, tag="o_vector", bufs=PIECES, name="o_vector"
+            )
             nc.gpsimd.tensor_scalar(
-                out=o_sb[(g, cb)][:],
-                in0=x_sb[g][:, cb, :],
+                out=o_vector[piece][:],
+                in0=x_even[g][:, pair, :],
                 scalar1=1.0,
-                scalar2=shift[:, cb : cb + 1],
+                scalar2=shift[:, 2 * pair : 2 * pair + 1],
                 op0=ALU.mult,
                 op1=ALU.add,
             )
 
         def project(piece):
-            g, cb_a, cb_b = blocks_of(piece)
-            for cb in (cb_a, cb_b):
+            g, pair = divmod(piece, PAIRS)
+            for parity in range(2):
+                cb = 2 * pair + parity
                 cols = slice(cb * P, (cb + 1) * P)
-                y_ps[(g, cb)] = psum.tile([P, GROUP_POS], F32, tag="y", bufs=2, name="y_ps")
+                y_ps[(piece, parity)] = psum.tile(
+                    [P, GROUP_POS], F32, tag="y", bufs=2, name="y_ps"
+                )
                 nc.tensor.matmul_mx(
-                    out=y_ps[(g, cb)][:],
+                    out=y_ps[(piece, parity)][:],
                     lhsT=wp_codes[:, cols].bitcast(FP8X4),
                     lhsT_scale=wp_scales[:, cols],
                     rhs=g_codes[g][:].bitcast(FP8X4),
@@ -264,43 +288,45 @@ def tile_selfattention_pb_kernel(
                     stop=True,
                 )
 
-        def finish(piece):
-            g, cb_v, cb_s = blocks_of(piece)
-            pos = slice(g * GROUP_POS, (g + 1) * GROUP_POS)
+        def finish_even_block(piece):
+            g, pair = divmod(piece, PAIRS)
+            cb = 2 * pair
             nc.vector.scalar_tensor_tensor(
-                out=o_sb[(g, cb_v)][:],
-                in0=y_ps[(g, cb_v)][:],
-                scalar=gain[:, cb_v : cb_v + 1],
-                in1=o_sb[(g, cb_v)][:],
+                out=o_vector[piece][:],
+                in0=y_ps[(piece, 0)][:],
+                scalar=gain[:, cb : cb + 1],
+                in1=o_vector[piece][:],
                 op0=ALU.mult,
                 op1=ALU.add,
             )
-            nc.sync.dma_start(out=out_view[:, cb_v, pos], in_=o_sb[(g, cb_v)][:])
+            nc.sync.dma_start(
+                out=out_view[:, 0, pair, g * GROUP_POS : (g + 1) * GROUP_POS],
+                in_=o_vector[piece][:],
+            )
+
+        def finish_odd_block(piece):
+            g, pair = divmod(piece, PAIRS)
+            cb = 2 * pair + 1
             o_scalar = work.tile([P, GROUP_POS], F32, tag="o_scalar", bufs=4)
             nc.scalar.activation(
                 out=o_scalar[:],
-                in_=y_ps[(g, cb_s)][:],
+                in_=y_ps[(piece, 1)][:],
                 func=ACT.Identity,
-                bias=shift[:, cb_s : cb_s + 1],
-                scale=gain[:, cb_s : cb_s + 1],
+                bias=shift[:, cb : cb + 1],
+                scale=gain[:, cb : cb + 1],
             )
             nc.gpsimd.tensor_tensor(
-                out=o_scalar[:], in0=o_scalar[:], in1=x_sb[g][:, cb_s, :], op=ALU.add
+                out=o_scalar[:], in0=o_scalar[:], in1=x_odd[g][:, pair, :], op=ALU.add
             )
-            nc.sync.dma_start(out=out_view[:, cb_s, pos], in_=o_scalar[:])
-
-        def regroup_v():
-            nc.vector.tensor_copy(
-                out=v_grouped[:].rearrange("p (t m) j -> p t m j", t=PACK),
-                in_=v_raw[:].rearrange("p j (m t) -> p t m j", t=PACK),
+            nc.sync.dma_start(
+                out=out_view[:, 1, pair, g * GROUP_POS : (g + 1) * GROUP_POS], in_=o_scalar[:]
             )
 
-        def quantise_v():
-            nc.vector.quantize_mx(
-                out=v_codes[:].bitcast(FP8X4),
-                scales=v_scales[:],
-                in_=v_grouped[:].rearrange("p c j -> p (c j)"),
-            )
+        def transpose_q(g, tag):
+            qT_ps = psum.tile([P, GROUP, P], BF16, tag=tag, bufs=2 if tag == "y" else 1)
+            for il in range(GROUP):
+                nc.tensor.transpose(qT_ps[:, il, :], q_raw[g][:, il, :], ident_bf[:])
+            return lambda: nc.scalar.copy(out=qT[g][:], in_=qT_ps[:])
 
         wp_words = wp_raw[:].bitcast(F32).rearrange("r b (p u) -> r b u p", u=2)
         wp_grouped_words = wp_grouped[:].bitcast(F32)
@@ -312,82 +338,120 @@ def tile_selfattention_pb_kernel(
                     nc.tensor.transpose(
                         wT_ps[:, c, u, :], wp_words[:, 2 * pair + c, u, :], ident_f32[:]
                     )
-            nc.vector.tensor_copy(
+            return lambda: nc.scalar.copy(
                 out=wp_grouped_words[:, 2 * pair * P : (2 * pair + 2) * P, :].rearrange(
                     "p (c r) u -> p c r u", c=2
                 ),
                 in_=wT_ps[:].rearrange("p c u r -> p c r u"),
             )
 
-        def quantise_wp(half):
-            rows = slice(half * OUT_CH // 2, (half + 1) * OUT_CH // 2)
+        def quantise_wp(pair):
+            rows = slice(2 * pair * P, (2 * pair + 2) * P)
             nc.vector.quantize_mx(
                 out=wp_codes[:, rows].bitcast(FP8X4),
                 scales=wp_scales[:, rows],
                 in_=wp_grouped[:, rows, :].rearrange("p r t -> p (r t)"),
             )
 
-        def channel_constants_first():
-            vec_ps = psum.tile([P, P], BF16, tag="r")
-            nc.tensor.transpose(vec_ps[:], vec_rows[:], ident_bf[:])
-            nc.vector.tensor_copy(out=vec_cols[:], in_=vec_ps[:, 0 : 5 * BLOCKS])
-            nc.vector.tensor_copy(out=gamma_f32[:], in_=gamma_bf[:])
-            nc.vector.tensor_scalar_add(
-                out=var_eps[:], in0=vec_cols[:, 4 * BLOCKS : 5 * BLOCKS], scalar1=EPS
+        def quantise_v():
+            nc.vector.quantize_mx(
+                out=v_codes[:].bitcast(FP8X4),
+                scales=v_scales[:],
+                in_=v_grouped[:].rearrange("p c j -> p (c j)"),
             )
-            nc.gpsimd.tensor_tensor(out=rstd[:], in0=var_eps[:], in1=neg_half[:], op=ALU.pow)
 
-        def channel_constants_second():
+        def transpose_vectors():
+            vec_ps = psum.tile([P, P], BF16, tag="y", bufs=2)
+            nc.tensor.transpose(vec_ps[:], vec_rows[:], ident_bf[:])
+            return lambda: channel_constants(vec_ps)
+
+        def channel_constants(vec_ps):
+            nc.scalar.copy(out=vec_cols[:], in_=vec_ps[:, 0 : 5 * BLOCKS])
             bias_c = vec_cols[:, 0:BLOCKS]
             gain_c = vec_cols[:, BLOCKS : 2 * BLOCKS]
             beta_c = vec_cols[:, 2 * BLOCKS : 3 * BLOCKS]
             mean_c = vec_cols[:, 3 * BLOCKS : 4 * BLOCKS]
-            nc.vector.tensor_tensor(out=centred[:], in0=bias_c, in1=mean_c, op=ALU.subtract)
-            nc.vector.tensor_tensor(out=inv[:], in0=gain_c, in1=rstd[:], op=ALU.mult)
-            nc.vector.tensor_scalar_mul(out=gain[:], in0=inv[:], scalar1=gamma_f32[:, 0:1])
-            nc.vector.tensor_tensor(out=scaled[:], in0=centred[:], in1=inv[:], op=ALU.mult)
-            nc.vector.tensor_tensor(out=shifted[:], in0=scaled[:], in1=beta_c, op=ALU.add)
-            nc.vector.tensor_scalar_mul(out=shift[:], in0=shifted[:], scalar1=gamma_f32[:, 0:1])
+            var_c = vec_cols[:, 4 * BLOCKS : 5 * BLOCKS]
+            pool = nc.gpsimd
+            pool.tensor_scalar(
+                out=var_eps[:], in0=var_c, scalar1=1.0, scalar2=EPS, op0=ALU.mult, op1=ALU.add
+            )
+            pool.tensor_tensor(out=rstd[:], in0=var_eps[:], in1=neg_half[:], op=ALU.pow)
+            pool.tensor_copy(out=gamma_f32[:], in_=gamma_bf[:])
+            pool.tensor_tensor(out=centred[:], in0=bias_c, in1=mean_c, op=ALU.subtract)
+            pool.tensor_tensor(out=inv[:], in0=gain_c, in1=rstd[:], op=ALU.mult)
+            pool.tensor_tensor(out=scaled[:], in0=centred[:], in1=inv[:], op=ALU.mult)
+            pool.tensor_tensor(out=shifted[:], in0=scaled[:], in1=beta_c, op=ALU.add)
+            pool.tensor_scalar(
+                out=shift[:],
+                in0=shifted[:],
+                scalar1=gamma_f32[:, 0:1],
+                scalar2=0.0,
+                op0=ALU.mult,
+                op1=ALU.add,
+            )
+            pool.tensor_scalar(
+                out=gain[:],
+                in0=inv[:],
+                scalar1=gamma_f32[:, 0:1],
+                scalar2=0.0,
+                op0=ALU.mult,
+                op1=ALU.add,
+            )
 
-        PROJECT_LAG = GROUP + 1
-        transpose_q(0)
+        FIRST_PIECE = GROUP + 2
+        X_AHEAD = 2
+        prepared = 0
+
+        def tile_in_range(i):
+            return 0 <= i < TILES
+
+        transpose_q(0, "tp")()
         scores(0)
-        for n in range(PIECES + PROJECT_LAG + 1):
-            if 1 <= n <= TILES:
-                reciprocal_of_sum(n - 1)
-            if n + 1 < TILES:
+        for n in range(FIRST_PIECE + PIECES):
+            piece = n - FIRST_PIECE
+            if tile_in_range(n):
+                row_maximum(n)
+            if tile_in_range(n + 1):
                 scores(n + 1)
-            if n < TILES:
-                softmax_numerator(n)
-            if n == 0:
-                regroup_v()
-            if n == 3:
-                channel_constants_second()
-            if 1 <= n <= TILES:
-                e_grouped = transpose_e(n - 1)
-            if n % GROUP == 1 and n // GROUP + 1 < GROUPS:
-                transpose_q(n // GROUP + 1)
-            if n == 2:
-                channel_constants_first()
-            if 2 <= n < 2 + BLOCKS // 2:
-                transpose_wp(n - 2)
-            if 2 <= n < TILES + 2:
-                g_ps = attend(n - 2)
-            if 0 <= n - PROJECT_LAG - 1 < PIECES:
-                finish(n - PROJECT_LAG - 1)
-            if 2 <= n < TILES + 2:
-                normalise(n - 2, g_ps)
             if n == 1:
                 quantise_v()
-            if 1 <= n <= TILES:
-                quantise_e(n - 1, e_grouped)
-            if 2 <= n < TILES + 2:
+            if 0 <= n - 3 < PAIRS:
+                quantise_wp(n - 3)
+            if tile_in_range(n - 2):
+                normalise(n - 2)
+            if piece >= 0:
+                project(piece)
+            if tile_in_range(n):
+                exponentials(n)
+            if tile_in_range(n - 1):
+                spread_reciprocals(n - 1)
+                quantise_e(n - 1)
+            if piece >= 0:
+                finish_even_block(piece)
+            if tile_in_range(n - 2):
                 quantise_g(n - 2)
-            if n == 4:
-                quantise_wp(0)
-            if n == 6:
-                quantise_wp(1)
-            if 0 <= n - PROJECT_LAG < PIECES:
-                project(n - PROJECT_LAG)
-            if 0 <= n - PROJECT_LAG + 2 < PIECES:
-                add_shift_to_x(n - PROJECT_LAG + 2)
+            for copy_out in waiting:
+                copy_out()
+            waiting = []
+            if tile_in_range(n):
+                reciprocal_of_sum(n)
+                transpose_e(n)
+            if tile_in_range(n - 1):
+                copy_reciprocals(n - 1)
+                attend(n - 1)
+            if n + 1 < GROUPS:
+                waiting.append(transpose_q(n + 1, "y"))
+            if n == 0:
+                waiting.append(transpose_vectors())
+            if 0 <= n - 1 < PAIRS:
+                waiting.append(transpose_wp(n - 1))
+            if piece >= 0:
+                finish_odd_block(piece)
+            if tile_in_range(n):
+                copy_e(n)
+            if n >= 2:
+                for ahead in range(X_AHEAD):
+                    if prepared < PIECES:
+                        add_shift_to_x(prepared)
+                        prepared += 1

@@ -70,16 +70,14 @@ def tile_selfattention_pb_kernel(
         load_q(0)
         nc.sync.dma_start(out=k_raw[:], in_=k.rearrange("b c n -> (b c) n"))
         nc.sync.dma_start(out=v_raw[:], in_=v.rearrange("b (p j) c -> p (b j) c", j=PACK))
-        nc.sync.dma_start(out=wp_raw[:], in_=wp.rearrange("(cb p) c -> p cb c", p=P))
-
         nc.vector.memset(vec_rows[:], 0.0)
         for j, vec in enumerate((bp, bnp_s, bnp_b, bnp_m, bnp_v)):
-            nc.scalar.dma_start(
+            nc.sync.dma_start(
                 out=vec_rows[j * BLOCKS : (j + 1) * BLOCKS, :],
                 in_=vec.rearrange("(cb p) -> cb p", p=P),
             )
-        nc.scalar.dma_start(out=gamma_bf[:], in_=gamma.partition_broadcast(P))
-
+        nc.sync.dma_start(out=gamma_bf[:], in_=gamma.partition_broadcast(P))
+        nc.sync.dma_start(out=wp_raw[:], in_=wp.rearrange("(cb p) c -> p cb c", p=P))
         for g in range(1, GROUPS):
             load_q(g)
         load_x(x_even, 0, 0)

@@ -128,15 +128,6 @@ def tile_selfattention_pb_kernel(
         gain = const.tile([P, BLOCKS], F32)
         shift = const.tile([P, BLOCKS], F32)
 
-        nc.gpsimd.tensor_scalar(
-            out=v_grouped[:].rearrange("p (t m) j -> p t m j", t=PACK),
-            in0=v_raw[:].rearrange("p j (m t) -> p t m j", t=PACK),
-            scalar1=1.0,
-            scalar2=0.0,
-            op0=ALU.mult,
-            op1=ALU.add,
-        )
-
         s_ps = {}
         e_bf = {}
         eT_ps = {}
@@ -351,6 +342,16 @@ def tile_selfattention_pb_kernel(
                 in_=wp_grouped[:, rows, :].rearrange("p r t -> p (r t)"),
             )
 
+        def regroup_v():
+            nc.gpsimd.tensor_scalar(
+                out=v_grouped[:].rearrange("p (t m) j -> p t m j", t=PACK),
+                in0=v_raw[:].rearrange("p j (m t) -> p t m j", t=PACK),
+                scalar1=1.0,
+                scalar2=0.0,
+                op0=ALU.mult,
+                op1=ALU.add,
+            )
+
         def quantise_v():
             nc.vector.quantize_mx(
                 out=v_codes[:].bitcast(FP8X4),
@@ -358,44 +359,30 @@ def tile_selfattention_pb_kernel(
                 in_=v_grouped[:].rearrange("p c j -> p (c j)"),
             )
 
-        def transpose_vectors():
+        def channel_constants():
             vec_ps = psum.tile([P, P], BF16, tag="y", bufs=2)
             nc.tensor.transpose(vec_ps[:], vec_rows[:], ident_bf[:])
-            return lambda: channel_constants(vec_ps)
-
-        def channel_constants(vec_ps):
-            nc.scalar.copy(out=vec_cols[:], in_=vec_ps[:, 0 : 5 * BLOCKS])
+            nc.vector.tensor_copy(out=vec_cols[:], in_=vec_ps[:, 0 : 5 * BLOCKS])
             bias_c = vec_cols[:, 0:BLOCKS]
             gain_c = vec_cols[:, BLOCKS : 2 * BLOCKS]
             beta_c = vec_cols[:, 2 * BLOCKS : 3 * BLOCKS]
             mean_c = vec_cols[:, 3 * BLOCKS : 4 * BLOCKS]
             var_c = vec_cols[:, 4 * BLOCKS : 5 * BLOCKS]
-            pool = nc.gpsimd
-            pool.tensor_scalar(
-                out=var_eps[:], in0=var_c, scalar1=1.0, scalar2=EPS, op0=ALU.mult, op1=ALU.add
-            )
-            pool.tensor_tensor(out=rstd[:], in0=var_eps[:], in1=neg_half[:], op=ALU.pow)
-            pool.tensor_copy(out=gamma_f32[:], in_=gamma_bf[:])
-            pool.tensor_tensor(out=centred[:], in0=bias_c, in1=mean_c, op=ALU.subtract)
-            pool.tensor_tensor(out=inv[:], in0=gain_c, in1=rstd[:], op=ALU.mult)
-            pool.tensor_tensor(out=scaled[:], in0=centred[:], in1=inv[:], op=ALU.mult)
-            pool.tensor_tensor(out=shifted[:], in0=scaled[:], in1=beta_c, op=ALU.add)
-            pool.tensor_scalar(
-                out=shift[:],
-                in0=shifted[:],
-                scalar1=gamma_f32[:, 0:1],
-                scalar2=0.0,
-                op0=ALU.mult,
-                op1=ALU.add,
-            )
-            pool.tensor_scalar(
-                out=gain[:],
-                in0=inv[:],
-                scalar1=gamma_f32[:, 0:1],
-                scalar2=0.0,
-                op0=ALU.mult,
-                op1=ALU.add,
-            )
+            nc.vector.tensor_scalar_add(out=var_eps[:], in0=var_c, scalar1=EPS)
+            nc.gpsimd.tensor_tensor(out=rstd[:], in0=var_eps[:], in1=neg_half[:], op=ALU.pow)
+            nc.vector.tensor_copy(out=gamma_f32[:], in_=gamma_bf[:])
+            nc.vector.tensor_tensor(out=centred[:], in0=bias_c, in1=mean_c, op=ALU.subtract)
+
+            def second_part():
+                nc.vector.tensor_tensor(out=inv[:], in0=gain_c, in1=rstd[:], op=ALU.mult)
+                nc.vector.tensor_scalar_mul(out=gain[:], in0=inv[:], scalar1=gamma_f32[:, 0:1])
+                nc.vector.tensor_tensor(out=scaled[:], in0=centred[:], in1=inv[:], op=ALU.mult)
+                nc.vector.tensor_tensor(out=shifted[:], in0=scaled[:], in1=beta_c, op=ALU.add)
+                nc.vector.tensor_scalar_mul(
+                    out=shift[:], in0=shifted[:], scalar1=gamma_f32[:, 0:1]
+                )
+
+            return second_part
 
         FIRST_PIECE = GROUP + 2
         X_AHEAD = 2
@@ -404,7 +391,10 @@ def tile_selfattention_pb_kernel(
         def tile_in_range(i):
             return 0 <= i < TILES
 
-        transpose_q(0, "tp")()
+        copy_q = transpose_q(0, "tp")
+        rest_of_constants = channel_constants()
+        regroup_v()
+        copy_q()
         scores(0)
         for n in range(FIRST_PIECE + PIECES):
             piece = n - FIRST_PIECE
@@ -412,6 +402,8 @@ def tile_selfattention_pb_kernel(
                 row_maximum(n)
             if tile_in_range(n + 1):
                 scores(n + 1)
+            if n == 0:
+                rest_of_constants()
             if n == 1:
                 quantise_v()
             if 0 <= n - 3 < PAIRS:
@@ -440,15 +432,13 @@ def tile_selfattention_pb_kernel(
                 attend(n - 1)
             if n + 1 < GROUPS:
                 waiting.append(transpose_q(n + 1, "y"))
-            if n == 0:
-                waiting.append(transpose_vectors())
             if 0 <= n - 1 < PAIRS:
                 waiting.append(transpose_wp(n - 1))
             if piece >= 0:
                 finish_odd_block(piece)
             if tile_in_range(n):
                 copy_e(n)
-            if n >= 2:
+            if n >= 1:
                 for ahead in range(X_AHEAD):
                     if prepared < PIECES:
                         add_shift_to_x(prepared)

@@ -128,6 +128,15 @@ def tile_selfattention_pb_kernel(
         gain = const.tile([P, BLOCKS], F32)
         shift = const.tile([P, BLOCKS], F32)
 
+        nc.gpsimd.tensor_scalar(
+            out=v_grouped[:].rearrange("p (t m) j -> p t m j", t=PACK),
+            in0=v_raw[:].rearrange("p j (m t) -> p t m j", t=PACK),
+            scalar1=1.0,
+            scalar2=0.0,
+            op0=ALU.mult,
+            op1=ALU.add,
+        )
+
         s_ps = {}
         e_bf = {}
         eT_ps = {}
@@ -205,7 +214,7 @@ def tile_selfattention_pb_kernel(
             )
 
         def attend(i):
-            g_ps[i] = psum.tile([P, PACK, P], F32, tag="g", bufs=2, name="g_ps")
+            g_ps[i] = psum.tile([P, PACK, P], F32, tag="g", bufs=1, name="g_ps")
             for t in range(PACK):
                 cols = slice(t * P, (t + 1) * P)
                 nc.tensor.matmul_mx(
@@ -265,7 +274,7 @@ def tile_selfattention_pb_kernel(
                 cb = 2 * pair + parity
                 cols = slice(cb * P, (cb + 1) * P)
                 y_ps[(piece, parity)] = psum.tile(
-                    [P, GROUP_POS], F32, tag="y", bufs=2, name="y_ps"
+                    [P, GROUP_POS], F32, tag="y", bufs=3, name="y_ps"
                 )
                 nc.tensor.matmul_mx(
                     out=y_ps[(piece, parity)][:],
@@ -312,7 +321,7 @@ def tile_selfattention_pb_kernel(
             )
 
         def transpose_q(g, tag):
-            qT_ps = psum.tile([P, GROUP, P], BF16, tag=tag, bufs=2 if tag == "y" else 1)
+            qT_ps = psum.tile([P, GROUP, P], BF16, tag=tag, bufs=3 if tag == "y" else 1)
             for il in range(GROUP):
                 nc.tensor.transpose(qT_ps[:, il, :], q_raw[g][:, il, :], ident_bf[:])
             return lambda: nc.scalar.copy(out=qT[g][:], in_=qT_ps[:])
@@ -321,7 +330,7 @@ def tile_selfattention_pb_kernel(
         wp_grouped_words = wp_grouped[:].bitcast(F32)
 
         def transpose_wp(pair):
-            wT_ps = psum.tile([P, 2, 2, P], F32, tag="y", bufs=2)
+            wT_ps = psum.tile([P, 2, 2, P], F32, tag="y", bufs=3)
             for c in range(2):
                 for u in range(2):
                     nc.tensor.transpose(
@@ -342,16 +351,6 @@ def tile_selfattention_pb_kernel(
                 in_=wp_grouped[:, rows, :].rearrange("p r t -> p (r t)"),
             )
 
-        def regroup_v():
-            nc.gpsimd.tensor_scalar(
-                out=v_grouped[:].rearrange("p (t m) j -> p t m j", t=PACK),
-                in0=v_raw[:].rearrange("p j (m t) -> p t m j", t=PACK),
-                scalar1=1.0,
-                scalar2=0.0,
-                op0=ALU.mult,
-                op1=ALU.add,
-            )
-
         def quantise_v():
             nc.vector.quantize_mx(
                 out=v_codes[:].bitcast(FP8X4),
@@ -359,30 +358,44 @@ def tile_selfattention_pb_kernel(
                 in_=v_grouped[:].rearrange("p c j -> p (c j)"),
             )
 
-        def channel_constants():
-            vec_ps = psum.tile([P, P], BF16, tag="y", bufs=2)
+        def transpose_vectors():
+            vec_ps = psum.tile([P, P], BF16, tag="y", bufs=3)
             nc.tensor.transpose(vec_ps[:], vec_rows[:], ident_bf[:])
-            nc.vector.tensor_copy(out=vec_cols[:], in_=vec_ps[:, 0 : 5 * BLOCKS])
+            return lambda: channel_constants(vec_ps)
+
+        def channel_constants(vec_ps):
+            nc.scalar.copy(out=vec_cols[:], in_=vec_ps[:, 0 : 5 * BLOCKS])
             bias_c = vec_cols[:, 0:BLOCKS]
             gain_c = vec_cols[:, BLOCKS : 2 * BLOCKS]
             beta_c = vec_cols[:, 2 * BLOCKS : 3 * BLOCKS]
             mean_c = vec_cols[:, 3 * BLOCKS : 4 * BLOCKS]
             var_c = vec_cols[:, 4 * BLOCKS : 5 * BLOCKS]
-            nc.vector.tensor_scalar_add(out=var_eps[:], in0=var_c, scalar1=EPS)
-            nc.gpsimd.tensor_tensor(out=rstd[:], in0=var_eps[:], in1=neg_half[:], op=ALU.pow)
-            nc.vector.tensor_copy(out=gamma_f32[:], in_=gamma_bf[:])
-            nc.vector.tensor_tensor(out=centred[:], in0=bias_c, in1=mean_c, op=ALU.subtract)
-
-            def second_part():
-                nc.vector.tensor_tensor(out=inv[:], in0=gain_c, in1=rstd[:], op=ALU.mult)
-                nc.vector.tensor_scalar_mul(out=gain[:], in0=inv[:], scalar1=gamma_f32[:, 0:1])
-                nc.vector.tensor_tensor(out=scaled[:], in0=centred[:], in1=inv[:], op=ALU.mult)
-                nc.vector.tensor_tensor(out=shifted[:], in0=scaled[:], in1=beta_c, op=ALU.add)
-                nc.vector.tensor_scalar_mul(
-                    out=shift[:], in0=shifted[:], scalar1=gamma_f32[:, 0:1]
-                )
-
-            return second_part
+            pool = nc.gpsimd
+            pool.tensor_scalar(
+                out=var_eps[:], in0=var_c, scalar1=1.0, scalar2=EPS, op0=ALU.mult, op1=ALU.add
+            )
+            pool.tensor_tensor(out=rstd[:], in0=var_eps[:], in1=neg_half[:], op=ALU.pow)
+            pool.tensor_copy(out=gamma_f32[:], in_=gamma_bf[:])
+            pool.tensor_tensor(out=centred[:], in0=bias_c, in1=mean_c, op=ALU.subtract)
+            pool.tensor_tensor(out=inv[:], in0=gain_c, in1=rstd[:], op=ALU.mult)
+            pool.tensor_tensor(out=scaled[:], in0=centred[:], in1=inv[:], op=ALU.mult)
+            pool.tensor_tensor(out=shifted[:], in0=scaled[:], in1=beta_c, op=ALU.add)
+            pool.tensor_scalar(
+                out=shift[:],
+                in0=shifted[:],
+                scalar1=gamma_f32[:, 0:1],
+                scalar2=0.0,
+                op0=ALU.mult,
+                op1=ALU.add,
+            )
+            pool.tensor_scalar(
+                out=gain[:],
+                in0=inv[:],
+                scalar1=gamma_f32[:, 0:1],
+                scalar2=0.0,
+                op0=ALU.mult,
+                op1=ALU.add,
+            )
 
         FIRST_PIECE = GROUP + 2
         X_AHEAD = 2
@@ -391,10 +404,7 @@ def tile_selfattention_pb_kernel(
         def tile_in_range(i):
             return 0 <= i < TILES
 
-        copy_q = transpose_q(0, "tp")
-        rest_of_constants = channel_constants()
-        regroup_v()
-        copy_q()
+        transpose_q(0, "tp")()
         scores(0)
         for n in range(FIRST_PIECE + PIECES):
             piece = n - FIRST_PIECE
@@ -402,8 +412,6 @@ def tile_selfattention_pb_kernel(
                 row_maximum(n)
             if tile_in_range(n + 1):
                 scores(n + 1)
-            if n == 0:
-                rest_of_constants()
             if n == 1:
                 quantise_v()
             if 0 <= n - 3 < PAIRS:
@@ -432,13 +440,15 @@ def tile_selfattention_pb_kernel(
                 attend(n - 1)
             if n + 1 < GROUPS:
                 waiting.append(transpose_q(n + 1, "y"))
+            if n == 0:
+                waiting.append(transpose_vectors())
             if 0 <= n - 1 < PAIRS:
                 waiting.append(transpose_wp(n - 1))
             if piece >= 0:
                 finish_odd_block(piece)
             if tile_in_range(n):
                 copy_e(n)
-            if n >= 1:
+            if n >= 2:
                 for ahead in range(X_AHEAD):
                     if prepared < PIECES:
                         add_shift_to_x(prepared)

@@ -99,8 +99,10 @@ def tile_selfattention_pb_kernel(
         nc.vector.memset(warm_in[:], 0.0)
         nc.scalar.activation(out=warm_out[:], in_=warm_in[:], func=ACT.Exp)
 
-        k_perm = const.tile([P, PACK, P], BF16)
-        nc.vector.tensor_copy(out=k_perm[:], in_=k_raw[:].rearrange("c (p t) -> c t p", t=PACK))
+        k_perm = const.tile([P, 2, P, 2], BF16)
+        nc.vector.tensor_copy(
+            out=k_perm[:], in_=k_raw[:].rearrange("c (p u two) -> c u p two", u=2, two=2)
+        )
 
         neg_max = const.tile([P, TILES], F32)
         row_sum = const.tile([P, TILES], F32)
@@ -159,7 +161,7 @@ def tile_selfattention_pb_kernel(
             nc.tensor.matmul(
                 s_ps[i][:],
                 lhsT=qT[g][:, il, :],
-                rhs=k_perm[:].rearrange("c t p -> c (t p)"),
+                rhs=k_perm[:].rearrange("c u p two -> c (u p two)"),
                 start=True,
                 stop=True,
             )
@@ -170,9 +172,9 @@ def tile_selfattention_pb_kernel(
             )
 
         def exponentials(i):
-            e_bf[i] = work.tile([P, PACK, P], BF16, tag="e_bf", name="e_bf")
+            e_bf[i] = work.tile([P, POOLED], BF16, tag="e_bf", name="e_bf")
             nc.scalar.activation(
-                out=e_bf[i][:].rearrange("r t p -> r (t p)"),
+                out=e_bf[i][:],
                 in_=s_ps[i][:],
                 func=ACT.Exp,
                 bias=neg_max[:, i : i + 1],
@@ -184,15 +186,20 @@ def tile_selfattention_pb_kernel(
             nc.vector.reciprocal(out=inv_sum[:, i : i + 1], in_=row_sum[:, i : i + 1])
 
         def transpose_e(i):
-            eT_ps[i] = psum.tile([P, PACK, P], BF16, tag="tp", name="eT_ps")
-            for t in range(PACK):
-                nc.tensor.transpose(eT_ps[i][:, t, :], e_bf[i][:, t, :], ident_bf[:])
+            eT_ps[i] = psum.tile([P, 2, P], F32, tag="tp", name="eT_ps")
+            e_words = e_bf[i][:].bitcast(F32)
+            for u in range(2):
+                nc.tensor.transpose(
+                    eT_ps[i][:, u, :], e_words[:, u * P : (u + 1) * P], ident_f32[:]
+                )
 
         def copy_e(i):
             e_grouped[i] = work.tile(
                 [P, P, PACK], BF16, tag="e_grouped", name="e_grouped", align_bytes=64
             )
-            nc.scalar.copy(out=e_grouped[i][:], in_=eT_ps[i][:].rearrange("p t r -> p r t"))
+            nc.scalar.copy(
+                out=e_grouped[i][:].bitcast(F32), in_=eT_ps[i][:].rearrange("p u r -> p r u")
+            )
 
         def spread_reciprocals(i):
             r_ps[i] = psum.tile([P, P], F32, tag="r", name="r_ps")

@@ -22,12 +22,23 @@ OUT_CH = 1024
 EPS = 1e-5
 
 TILES = POSITIONS // P
-GROUP = 4
-GROUP_POS = GROUP * P
-GROUPS = TILES // GROUP
+Q_PARTS = 4
+Q_TILES = TILES // Q_PARTS
 BLOCKS = OUT_CH // P
-PAIRS = BLOCKS // 2
-PIECES = GROUPS * PAIRS
+WP_PARTS = BLOCKS // 2
+X_PARTS = 2
+X_POS = POSITIONS // X_PARTS
+GROUP_TILES = (4, 4, 4, 2, 2)
+GROUPS = len(GROUP_TILES)
+GROUP_FIRST = [sum(GROUP_TILES[:g]) for g in range(GROUPS)]
+GROUP_OF = [g for g in range(GROUPS) for tile in range(GROUP_TILES[g])]
+LONG_PLAN = (((0,), (4,)), ((1,), (5,)), ((2,), (6,)), ((3,), (7,)))
+SHORT_PLAN = (((0, 1), (4, 5)), ((2, 3), (6, 7)))
+OUTPUT_PLAN = (LONG_PLAN, LONG_PLAN, LONG_PLAN, SHORT_PLAN)
+LAST_VECTOR = (0, 1, 2, 3, 4, 5)
+LAST_SCALAR = (6, 7)
+SHIFTS = tuple((cb, 0, 8) for cb in range(4)) + tuple((cb, 8, 16) for cb in range(4)) + ((4, 14, 16), (5, 14, 16))
+SHIFTED_BLOCKS = 6
 
 FLOPS = 2 * POSITIONS * POOLED * (QUERY_CH + VALUE_CH) + 2 * OUT_CH * VALUE_CH * POSITIONS
 
@@ -43,33 +54,30 @@ def tile_selfattention_pb_kernel(
         psum = ctx.enter_context(tc.psum_pool(name="psum", bufs=1))
 
         q_view = q.rearrange("b (i p) c -> p (b i) c", p=P)
-        x_view = x.rearrange("b (pair two p) h w -> p two (b pair) (h w)", two=2, p=P)
-        out_view = out.rearrange("b (pair two p) h w -> p two (b pair) (h w)", two=2, p=P)
+        x_view = x.rearrange("b (cb p) h w -> p (b cb) (h w)", p=P)
+        out_view = out.rearrange("b (cb p) h w -> p (b cb) (h w)", p=P)
 
-        q_raw = []
-        x_even = []
-        x_odd = []
-        for g in range(GROUPS):
-            q_raw.append(const.tile([P, GROUP, QUERY_CH], BF16, name="q_raw%d" % g))
-            x_even.append(const.tile([P, PAIRS, GROUP_POS], BF16, name="x_even%d" % g))
-            x_odd.append(const.tile([P, PAIRS, GROUP_POS], BF16, name="x_odd%d" % g))
+        q_first = const.tile([P, Q_TILES, QUERY_CH], BF16)
+        q_rest = const.tile([P, TILES - Q_TILES, QUERY_CH], BF16)
+        x_raw = []
+        for h in range(X_PARTS):
+            x_raw.append(const.tile([P, BLOCKS, X_POS], BF16, name="x_raw%d" % h))
+        x_shifted = const.tile([P, SHIFTED_BLOCKS, POSITIONS], F32)
         k_raw = const.tile([P, POOLED], BF16)
         v_raw = const.tile([P, PACK, VALUE_CH], BF16)
         wp_raw = const.tile([P, BLOCKS, VALUE_CH], BF16)
         vec_rows = const.tile([P, P], BF16)
         gamma_bf = const.tile([P, 1], BF16)
 
-        def load_q(g):
-            nc.sync.dma_start(out=q_raw[g][:], in_=q_view[:, g * GROUP : (g + 1) * GROUP, :])
-
-        def load_x(tiles, parity, g):
+        def load_x(h, blocks):
             nc.sync.dma_start(
-                out=tiles[g][:], in_=x_view[:, parity, :, g * GROUP_POS : (g + 1) * GROUP_POS]
+                out=x_raw[h][:, blocks, :], in_=x_view[:, blocks, h * X_POS : (h + 1) * X_POS]
             )
 
-        load_q(0)
+        nc.sync.dma_start(out=q_first[:], in_=q_view[:, 0:Q_TILES, :])
         nc.sync.dma_start(out=k_raw[:], in_=k.rearrange("b c n -> (b c) n"))
         nc.sync.dma_start(out=v_raw[:], in_=v.rearrange("b (p j) c -> p (b j) c", j=PACK))
+        nc.sync.dma_start(out=q_rest[:], in_=q_view[:, Q_TILES:TILES, :])
         nc.vector.memset(vec_rows[:], 0.0)
         for j, vec in enumerate((bp, bnp_s, bnp_b, bnp_m, bnp_v)):
             nc.sync.dma_start(
@@ -78,14 +86,9 @@ def tile_selfattention_pb_kernel(
             )
         nc.sync.dma_start(out=gamma_bf[:], in_=gamma.partition_broadcast(P))
         nc.sync.dma_start(out=wp_raw[:], in_=wp.rearrange("(cb p) c -> p cb c", p=P))
-        for g in range(1, GROUPS):
-            load_q(g)
-        load_x(x_even, 0, 0)
-        load_x(x_even, 0, 1)
-        for g in range(GROUPS):
-            load_x(x_odd, 1, g)
-            if g + 2 < GROUPS:
-                load_x(x_even, 0, g + 2)
+        for h in range(X_PARTS):
+            load_x(h, slice(0, 3))
+            load_x(h, slice(3, BLOCKS))
 
         ident_bf = const.tile([P, P], BF16)
         make_identity(nc, ident_bf[:])
@@ -109,8 +112,8 @@ def tile_selfattention_pb_kernel(
         inv_sum = const.tile([P, TILES], F32)
 
         qT = []
-        for g in range(GROUPS):
-            qT.append(const.tile([P, GROUP, P], BF16, name="qT%d" % g))
+        for part in range(Q_PARTS):
+            qT.append(const.tile([P, Q_TILES, P], BF16, name="qT%d" % part))
 
         v_grouped = const.tile([P, VALUE_CH, PACK], BF16, align_bytes=64)
         v_codes = const.tile([P, VALUE_CH], U32, align_bytes=64)
@@ -139,6 +142,12 @@ def tile_selfattention_pb_kernel(
             op1=ALU.add,
         )
 
+        g_codes = const.tile([P, POSITIONS], U32, align_bytes=64)
+        g_scales = const.tile([P, POSITIONS], U8, align_bytes=64)
+
+        def slot(i, count=1):
+            return slice(i * P, (i + count) * P)
+
         s_ps = {}
         e_bf = {}
         eT_ps = {}
@@ -149,18 +158,16 @@ def tile_selfattention_pb_kernel(
         r_sb = {}
         g_ps = {}
         g_grouped = {}
-        g_codes = {}
-        g_scales = {}
         y_ps = {}
-        o_vector = {}
+        o_scalar = {}
         waiting = []
 
         def scores(i):
-            g, il = divmod(i, GROUP)
+            part, il = divmod(i, Q_TILES)
             s_ps[i] = psum.tile([P, POOLED], F32, tag="s", bufs=2, name="s_ps")
             nc.tensor.matmul(
                 s_ps[i][:],
-                lhsT=qT[g][:, il, :],
+                lhsT=qT[part][:, il, :],
                 rhs=k_perm[:].rearrange("c u p two -> c (u p two)"),
                 start=True,
                 stop=True,
@@ -246,92 +253,101 @@ def tile_selfattention_pb_kernel(
             )
 
         def quantise_g(i):
-            g, il = divmod(i, GROUP)
-            if il == 0:
-                g_codes[g] = work.tile(
-                    [P, GROUP_POS], U32, tag="g_codes", name="g_codes", align_bytes=64
-                )
-                g_scales[g] = work.tile(
-                    [P, GROUP_POS], U8, tag="g_scales", name="g_scales", align_bytes=64
-                )
-            cols = slice(il * P, (il + 1) * P)
             nc.vector.quantize_mx(
-                out=g_codes[g][:, cols].bitcast(FP8X4),
-                scales=g_scales[g][:, cols],
+                out=g_codes[:, slot(i)].bitcast(FP8X4),
+                scales=g_scales[:, slot(i)],
                 in_=g_grouped[i][:].rearrange("p r t -> p (r t)"),
             )
 
-        def add_shift_to_x(piece):
-            g, pair = divmod(piece, PAIRS)
-            o_vector[piece] = work.tile(
-                [P, GROUP_POS], F32, tag="o_vector", bufs=PIECES, name="o_vector"
-            )
+        def group_columns(g):
+            first = GROUP_FIRST[g] * P
+            return slice(first, first + GROUP_TILES[g] * P)
+
+        def x_part(blocks, low, high):
+            h = low // X_POS
+            return x_raw[h][:, blocks, low - h * X_POS : high - h * X_POS]
+
+        def add_shift_to_x(cb, first_tile, last_tile):
+            low, high = first_tile * P, last_tile * P
             nc.gpsimd.tensor_scalar(
-                out=o_vector[piece][:],
-                in0=x_even[g][:, pair, :],
+                out=x_shifted[:, cb, low:high],
+                in0=x_part(cb, low, high),
                 scalar1=1.0,
-                scalar2=shift[:, 2 * pair : 2 * pair + 1],
+                scalar2=shift[:, cb : cb + 1],
                 op0=ALU.mult,
                 op1=ALU.add,
             )
 
-        def project(piece):
-            g, pair = divmod(piece, PAIRS)
-            for parity in range(2):
-                cb = 2 * pair + parity
-                cols = slice(cb * P, (cb + 1) * P)
-                y_ps[(piece, parity)] = psum.tile(
-                    [P, GROUP_POS], F32, tag="y", bufs=3, name="y_ps"
-                )
-                nc.tensor.matmul_mx(
-                    out=y_ps[(piece, parity)][:],
-                    lhsT=wp_codes[:, cols].bitcast(FP8X4),
-                    lhsT_scale=wp_scales[:, cols],
-                    rhs=g_codes[g][:].bitcast(FP8X4),
-                    rhs_scale=g_scales[g][:],
-                    start=True,
-                    stop=True,
-                )
+        def project(g, cb, tag="y", bufs=3):
+            cols = slice(cb * P, (cb + 1) * P)
+            positions = slot(GROUP_FIRST[g], GROUP_TILES[g])
+            y_ps[(g, cb)] = psum.tile(
+                [P, GROUP_TILES[g] * P], F32, tag=tag, bufs=bufs, name="y_ps"
+            )
+            nc.tensor.matmul_mx(
+                out=y_ps[(g, cb)][:],
+                lhsT=wp_codes[:, cols].bitcast(FP8X4),
+                lhsT_scale=wp_scales[:, cols],
+                rhs=g_codes[:, positions].bitcast(FP8X4),
+                rhs_scale=g_scales[:, positions],
+                start=True,
+                stop=True,
+            )
 
-        def finish_even_block(piece):
-            g, pair = divmod(piece, PAIRS)
-            cb = 2 * pair
+        def finish_on_vector(g, cb):
+            cols = group_columns(g)
             nc.vector.scalar_tensor_tensor(
-                out=o_vector[piece][:],
-                in0=y_ps[(piece, 0)][:],
+                out=x_shifted[:, cb, cols],
+                in0=y_ps[(g, cb)][:],
                 scalar=gain[:, cb : cb + 1],
-                in1=o_vector[piece][:],
+                in1=x_shifted[:, cb, cols],
                 op0=ALU.mult,
                 op1=ALU.add,
             )
+
+        def store_vector(g, first, last):
+            cols = group_columns(g)
             nc.sync.dma_start(
-                out=out_view[:, 0, pair, g * GROUP_POS : (g + 1) * GROUP_POS],
-                in_=o_vector[piece][:],
+                out=out_view[:, first:last, cols], in_=x_shifted[:, first:last, cols]
             )
 
-        def finish_odd_block(piece):
-            g, pair = divmod(piece, PAIRS)
-            cb = 2 * pair + 1
-            o_scalar = work.tile([P, GROUP_POS], F32, tag="o_scalar", bufs=4)
-            nc.scalar.activation(
-                out=o_scalar[:],
-                in_=y_ps[(piece, 1)][:],
-                func=ACT.Identity,
-                bias=shift[:, cb : cb + 1],
-                scale=gain[:, cb : cb + 1],
+        def scale_on_scalar(g, blocks):
+            o_scalar[(g, blocks)] = work.tile(
+                [P, len(blocks), GROUP_TILES[g] * P], F32, tag="o_scalar", name="o_scalar", bufs=10
             )
-            nc.gpsimd.tensor_tensor(
-                out=o_scalar[:], in0=o_scalar[:], in1=x_odd[g][:, pair, :], op=ALU.add
-            )
-            nc.sync.dma_start(
-                out=out_view[:, 1, pair, g * GROUP_POS : (g + 1) * GROUP_POS], in_=o_scalar[:]
+            for j, cb in enumerate(blocks):
+                nc.scalar.activation(
+                    out=o_scalar[(g, blocks)][:, j, :],
+                    in_=y_ps[(g, cb)][:],
+                    func=ACT.Identity,
+                    bias=shift[:, cb : cb + 1],
+                    scale=gain[:, cb : cb + 1],
+                )
+
+        def add_x(g, blocks, engine):
+            cols = group_columns(g)
+            engine.tensor_tensor(
+                out=o_scalar[(g, blocks)][:],
+                in0=o_scalar[(g, blocks)][:],
+                in1=x_part(slice(blocks[0], blocks[-1] + 1), cols.start, cols.stop),
+                op=ALU.add,
             )
 
-        def transpose_q(g, tag):
-            qT_ps = psum.tile([P, GROUP, P], BF16, tag=tag, bufs=3 if tag == "y" else 1)
-            for il in range(GROUP):
-                nc.tensor.transpose(qT_ps[:, il, :], q_raw[g][:, il, :], ident_bf[:])
-            return lambda: nc.scalar.copy(out=qT[g][:], in_=qT_ps[:])
+        def store_scalar(g, blocks):
+            nc.sync.dma_start(
+                out=out_view[:, blocks[0] : blocks[-1] + 1, group_columns(g)],
+                in_=o_scalar[(g, blocks)][:],
+            )
+
+        def transpose_q(part, tag):
+            qT_ps = psum.tile([P, Q_TILES, P], BF16, tag=tag, bufs=3 if tag == "y" else 1)
+            for il in range(Q_TILES):
+                if part == 0:
+                    q_tile = q_first[:, il, :]
+                else:
+                    q_tile = q_rest[:, (part - 1) * Q_TILES + il, :]
+                nc.tensor.transpose(qT_ps[:, il, :], q_tile, ident_bf[:])
+            return lambda: nc.scalar.copy(out=qT[part][:], in_=qT_ps[:])
 
         wp_words = wp_raw[:].bitcast(F32).rearrange("r b (p u) -> r b u p", u=2)
         wp_grouped_words = wp_grouped[:].bitcast(F32)
@@ -404,59 +420,104 @@ def tile_selfattention_pb_kernel(
                 op1=ALU.add,
             )
 
-        FIRST_PIECE = GROUP + 2
-        X_AHEAD = 2
-        prepared = 0
+        LAG = 2
 
         def tile_in_range(i):
             return 0 <= i < TILES
 
+        vector_work = {}
+        scalar_work = {}
+        for g in range(len(OUTPUT_PLAN)):
+            for s in range(len(OUTPUT_PLAN[g])):
+                step = GROUP_FIRST[g] + GROUP_TILES[g] + LAG + s
+                vector_blocks, scalar_blocks = OUTPUT_PLAN[g][s]
+                vector_work.setdefault(step, []).extend((g, cb) for cb in vector_blocks)
+                scalar_work.setdefault(step, []).append((g, scalar_blocks))
+        FIRST_SHIFT = 2
+        WP_TRANS = 2
+        WP_QUANT = 4
+        to_store = []
+
         transpose_q(0, "tp")()
         scores(0)
-        for n in range(FIRST_PIECE + PIECES):
-            piece = n - FIRST_PIECE
+        for n in range(TILES + LAG):
+            on_vector = vector_work.get(n, [])
+            on_scalar = scalar_work.get(n, [])
             if tile_in_range(n):
                 row_maximum(n)
             if tile_in_range(n + 1):
                 scores(n + 1)
+            if tile_in_range(n - 1):
+                reciprocal_of_sum(n - 1)
             if n == 1:
                 quantise_v()
-            if 0 <= n - 3 < PAIRS:
-                quantise_wp(n - 3)
+            if 0 <= n - WP_QUANT < WP_PARTS:
+                quantise_wp(n - WP_QUANT)
             if tile_in_range(n - 2):
                 normalise(n - 2)
-            if piece >= 0:
-                project(piece)
+            for g, cb in on_vector[:1] + [(g, blocks[0]) for g, blocks in on_scalar[:1]]:
+                project(g, cb)
             if tile_in_range(n):
                 exponentials(n)
             if tile_in_range(n - 1):
                 spread_reciprocals(n - 1)
+            if tile_in_range(n - 1):
                 quantise_e(n - 1)
-            if piece >= 0:
-                finish_even_block(piece)
+            for g, cb in on_vector:
+                if (g, cb) not in y_ps:
+                    project(g, cb)
+                finish_on_vector(g, cb)
+            for g in sorted({g for g, cb in on_vector}):
+                mine = [cb for h, cb in on_vector if h == g]
+                store_vector(g, mine[0], mine[-1] + 1)
             if tile_in_range(n - 2):
                 quantise_g(n - 2)
             for copy_out in waiting:
                 copy_out()
             waiting = []
-            if tile_in_range(n):
-                reciprocal_of_sum(n)
-                transpose_e(n)
             if tile_in_range(n - 1):
                 copy_reciprocals(n - 1)
+            if tile_in_range(n - 1):
                 attend(n - 1)
-            if n + 1 < GROUPS:
-                waiting.append(transpose_q(n + 1, "y"))
+            if tile_in_range(n):
+                transpose_e(n)
+            if n in (1, 3, 5):
+                waiting.append(transpose_q((n + 1) // 2, "y"))
             if n == 0:
                 waiting.append(transpose_vectors())
-            if 0 <= n - 1 < PAIRS:
-                waiting.append(transpose_wp(n - 1))
-            if piece >= 0:
-                finish_odd_block(piece)
+            if 0 <= n - WP_TRANS < WP_PARTS:
+                waiting.append(transpose_wp(n - WP_TRANS))
+            for g, blocks in on_scalar:
+                for cb in blocks:
+                    if (g, cb) not in y_ps:
+                        project(g, cb)
+                scale_on_scalar(g, blocks)
+                add_x(g, blocks, nc.gpsimd)
+            for g, blocks in to_store:
+                store_scalar(g, blocks)
+            to_store = on_scalar
             if tile_in_range(n):
                 copy_e(n)
-            if n >= 2:
-                for ahead in range(X_AHEAD):
-                    if prepared < PIECES:
-                        add_shift_to_x(prepared)
-                        prepared += 1
+            if 0 <= n - FIRST_SHIFT < len(SHIFTS):
+                add_shift_to_x(*SHIFTS[n - FIRST_SHIFT])
+
+        g = GROUPS - 1
+        banks = [("y", 3), ("s", 2), ("y", 3), ("s", 2), ("y", 3), ("tp", 1), ("r", 1), ("g", 1)]
+        order = []
+        for j in range(len(LAST_VECTOR)):
+            order.extend(LAST_SCALAR[j : j + 1] + LAST_VECTOR[j : j + 1])
+        for cb, (tag, bufs) in zip(order, banks):
+            project(g, cb, tag, bufs)
+        for cb in LAST_SCALAR:
+            scale_on_scalar(g, (cb,))
+        for cb in LAST_SCALAR[:-1]:
+            add_x(g, (cb,), nc.gpsimd)
+        for cb in LAST_VECTOR:
+            finish_on_vector(g, cb)
+        store_vector(g, 0, 3)
+        for pair in to_store:
+            store_scalar(*pair)
+        store_vector(g, 3, 6)
+        add_x(g, LAST_SCALAR[-1:], nc.vector)
+        for cb in LAST_SCALAR[-1:] + LAST_SCALAR[:-1]:
+            store_scalar(g, (cb,))

@@ -37,7 +37,7 @@ SHORT_PLAN = (((0, 1), (4, 5)), ((2, 3), (6, 7)))
 OUTPUT_PLAN = (LONG_PLAN, LONG_PLAN, LONG_PLAN, SHORT_PLAN)
 LAST_VECTOR = (0, 1, 2, 3, 4, 5)
 LAST_SCALAR = (6, 7)
-SHIFTS = tuple((cb, 0, 8) for cb in range(4)) + tuple((cb, 8, 16) for cb in range(4)) + ((4, 14, 16), (5, 14, 16))
+SHIFTS = tuple((cb, g, g + 4) for g in (0, 4, 8, 12) for cb in range(4)) + ((4, 14, 16), (5, 14, 16))
 SHIFTED_BLOCKS = 6
 
 FLOPS = 2 * POSITIONS * POOLED * (QUERY_CH + VALUE_CH) + 2 * OUT_CH * VALUE_CH * POSITIONS
@@ -420,7 +420,7 @@ def tile_selfattention_pb_kernel(
                 op1=ALU.add,
             )
 
-        LAG = 2
+        LAG = 3
 
         def tile_in_range(i):
             return 0 <= i < TILES
@@ -443,26 +443,26 @@ def tile_selfattention_pb_kernel(
         for n in range(TILES + LAG):
             on_vector = vector_work.get(n, [])
             on_scalar = scalar_work.get(n, [])
-            if tile_in_range(n):
-                row_maximum(n)
             if tile_in_range(n + 1):
                 scores(n + 1)
+            if tile_in_range(n):
+                row_maximum(n)
             if tile_in_range(n - 1):
                 reciprocal_of_sum(n - 1)
+            if tile_in_range(n - 3):
+                normalise(n - 3)
             if n == 1:
                 quantise_v()
             if 0 <= n - WP_QUANT < WP_PARTS:
                 quantise_wp(n - WP_QUANT)
             if tile_in_range(n - 2):
-                normalise(n - 2)
+                quantise_e(n - 2)
             for g, cb in on_vector[:1] + [(g, blocks[0]) for g, blocks in on_scalar[:1]]:
                 project(g, cb)
-            if tile_in_range(n):
-                exponentials(n)
+            if tile_in_range(n - 2):
+                spread_reciprocals(n - 2)
             if tile_in_range(n - 1):
-                spread_reciprocals(n - 1)
-            if tile_in_range(n - 1):
-                quantise_e(n - 1)
+                transpose_e(n - 1)
             for g, cb in on_vector:
                 if (g, cb) not in y_ps:
                     project(g, cb)
@@ -470,36 +470,37 @@ def tile_selfattention_pb_kernel(
             for g in sorted({g for g, cb in on_vector}):
                 mine = [cb for h, cb in on_vector if h == g]
                 store_vector(g, mine[0], mine[-1] + 1)
+            if tile_in_range(n):
+                exponentials(n)
             if tile_in_range(n - 2):
-                quantise_g(n - 2)
+                copy_reciprocals(n - 2)
+            if tile_in_range(n - 3):
+                quantise_g(n - 3)
             for copy_out in waiting:
                 copy_out()
             waiting = []
             if tile_in_range(n - 1):
-                copy_reciprocals(n - 1)
-            if tile_in_range(n - 1):
-                attend(n - 1)
-            if tile_in_range(n):
-                transpose_e(n)
-            if n in (1, 3, 5):
-                waiting.append(transpose_q((n + 1) // 2, "y"))
-            if n == 0:
-                waiting.append(transpose_vectors())
-            if 0 <= n - WP_TRANS < WP_PARTS:
-                waiting.append(transpose_wp(n - WP_TRANS))
+                copy_e(n - 1)
+            if tile_in_range(n - 2):
+                attend(n - 2)
+            for g, blocks in to_store:
+                store_scalar(g, blocks)
+            to_store = on_scalar
             for g, blocks in on_scalar:
                 for cb in blocks:
                     if (g, cb) not in y_ps:
                         project(g, cb)
                 scale_on_scalar(g, blocks)
                 add_x(g, blocks, nc.gpsimd)
-            for g, blocks in to_store:
-                store_scalar(g, blocks)
-            to_store = on_scalar
-            if tile_in_range(n):
-                copy_e(n)
-            if 0 <= n - FIRST_SHIFT < len(SHIFTS):
-                add_shift_to_x(*SHIFTS[n - FIRST_SHIFT])
+            if n >= FIRST_SHIFT:
+                for item in SHIFTS[2 * (n - FIRST_SHIFT) : 2 * (n - FIRST_SHIFT) + 2]:
+                    add_shift_to_x(*item)
+            if n in (1, 3, 5):
+                waiting.append(transpose_q((n + 1) // 2, "y"))
+            if n == 0:
+                waiting.append(transpose_vectors())
+            if 0 <= n - WP_TRANS < WP_PARTS:
+                waiting.append(transpose_wp(n - WP_TRANS))
 
         g = GROUPS - 1
         banks = [("y", 3), ("s", 2), ("y", 3), ("s", 2), ("y", 3), ("tp", 1), ("r", 1), ("g", 1)]

@@ -32,13 +32,13 @@ GROUP_TILES = (4, 4, 4, 2, 2)
 GROUPS = len(GROUP_TILES)
 GROUP_FIRST = [sum(GROUP_TILES[:g]) for g in range(GROUPS)]
 GROUP_OF = [g for g in range(GROUPS) for tile in range(GROUP_TILES[g])]
-LONG_PLAN = (((0,), (4,)), ((1,), (5,)), ((2,), (6,)), ((3,), (7,)))
-SHORT_PLAN = (((0, 1), (4, 5)), ((2, 3), (6, 7)))
+LONG_PLAN = (((0, 1), ()), ((2, 3), ()), ((4, 5), ()), ((6, 7), ()))
+SHORT_PLAN = (((0, 1, 2, 3), ()), ((4, 5, 6, 7), ()))
 OUTPUT_PLAN = (LONG_PLAN, LONG_PLAN, LONG_PLAN, SHORT_PLAN)
 LAST_VECTOR = (0, 1, 2, 3, 4, 5)
 LAST_SCALAR = (6, 7)
-SHIFTS = tuple((cb, g, g + 4) for g in (0, 4, 8, 12) for cb in range(4)) + ((4, 14, 16), (5, 14, 16))
-SHIFTED_BLOCKS = 6
+SHIFTS = tuple((cb, g, g + 4) for g in (0, 4, 8, 12) for cb in range(8))
+SHIFTED_BLOCKS = 8
 
 FLOPS = 2 * POSITIONS * POOLED * (QUERY_CH + VALUE_CH) + 2 * OUT_CH * VALUE_CH * POSITIONS
 
@@ -267,7 +267,7 @@ def tile_selfattention_pb_kernel(
             h = low // X_POS
             return x_raw[h][:, blocks, low - h * X_POS : high - h * X_POS]
 
-        def add_shift_to_x(cb, first_tile, last_tile):
+        def add_shift_on_gpsimd(cb, first_tile, last_tile):
             low, high = first_tile * P, last_tile * P
             nc.gpsimd.tensor_scalar(
                 out=x_shifted[:, cb, low:high],
@@ -276,6 +276,16 @@ def tile_selfattention_pb_kernel(
                 scalar2=shift[:, cb : cb + 1],
                 op0=ALU.mult,
                 op1=ALU.add,
+            )
+
+        def add_shift_on_scalar(cb, first_tile, last_tile):
+            low, high = first_tile * P, last_tile * P
+            nc.scalar.activation(
+                out=x_shifted[:, cb, low:high],
+                in_=x_part(cb, low, high),
+                func=ACT.Identity,
+                bias=shift[:, cb : cb + 1],
+                scale=1.0,
             )
 
         def project(g, cb, tag="y", bufs=3):
@@ -433,7 +443,12 @@ def tile_selfattention_pb_kernel(
                 vector_blocks, scalar_blocks = OUTPUT_PLAN[g][s]
                 vector_work.setdefault(step, []).extend((g, cb) for cb in vector_blocks)
                 scalar_work.setdefault(step, []).append((g, scalar_blocks))
-        FIRST_SHIFT = 2
+        GPSIMD_BY_STEP = {}
+        for j, item in enumerate(SHIFTS[:10]):
+            GPSIMD_BY_STEP.setdefault(2 + j // 2, []).append(item)
+        SCALAR_BY_STEP = {}
+        for j, item in enumerate(SHIFTS[10:]):
+            SCALAR_BY_STEP.setdefault(6 + j * 11 // 22, []).append(item)
         WP_TRANS = 2
         WP_QUANT = 4
         to_store = []
@@ -442,7 +457,7 @@ def tile_selfattention_pb_kernel(
         scores(0)
         for n in range(TILES + LAG):
             on_vector = vector_work.get(n, [])
-            on_scalar = scalar_work.get(n, [])
+            on_scalar = [item for item in scalar_work.get(n, []) if item[1]]
             if tile_in_range(n + 1):
                 scores(n + 1)
             if tile_in_range(n):
@@ -486,21 +501,22 @@ def tile_selfattention_pb_kernel(
             for g, blocks in to_store:
                 store_scalar(g, blocks)
             to_store = on_scalar
-            for g, blocks in on_scalar:
-                for cb in blocks:
-                    if (g, cb) not in y_ps:
-                        project(g, cb)
-                scale_on_scalar(g, blocks)
-                add_x(g, blocks, nc.gpsimd)
-            if n >= FIRST_SHIFT:
-                for item in SHIFTS[2 * (n - FIRST_SHIFT) : 2 * (n - FIRST_SHIFT) + 2]:
-                    add_shift_to_x(*item)
             if n in (1, 3, 5):
                 waiting.append(transpose_q((n + 1) // 2, "y"))
             if n == 0:
                 waiting.append(transpose_vectors())
             if 0 <= n - WP_TRANS < WP_PARTS:
                 waiting.append(transpose_wp(n - WP_TRANS))
+            for item in GPSIMD_BY_STEP.get(n, ()):
+                add_shift_on_gpsimd(*item)
+            for item in SCALAR_BY_STEP.get(n, ()):
+                add_shift_on_scalar(*item)
+            for g, blocks in on_scalar:
+                for cb in blocks:
+                    if (g, cb) not in y_ps:
+                        project(g, cb)
+                scale_on_scalar(g, blocks)
+                add_x(g, blocks, nc.gpsimd)
 
         g = GROUPS - 1
         banks = [("y", 3), ("s", 2), ("y", 3), ("s", 2), ("y", 3), ("tp", 1), ("r", 1), ("g", 1)]
@@ -516,8 +532,6 @@ def tile_selfattention_pb_kernel(
         for cb in LAST_VECTOR:
             finish_on_vector(g, cb)
         store_vector(g, 0, 3)
-        for pair in to_store:
-            store_scalar(*pair)
         store_vector(g, 3, 6)
         add_x(g, LAST_SCALAR[-1:], nc.vector)
         for cb in LAST_SCALAR[-1:] + LAST_SCALAR[:-1]:

@@ -53,7 +53,7 @@ def tile_selfattention_pb_kernel(
         work = ctx.enter_context(tc.tile_pool(name="work", bufs=3))
         psum = ctx.enter_context(tc.psum_pool(name="psum", bufs=1))
 
-        q_view = q.rearrange("b (i p) c -> p (b i) c", p=P)
+        q_view = q.rearrange("b (part p i) c -> p (b part) i c", p=P, i=Q_TILES)
         x_view = x.rearrange("b (cb p) h w -> p (b cb) (h w)", p=P)
         out_view = out.rearrange("b (cb p) h w -> p (b cb) (h w)", p=P)
 
@@ -74,10 +74,13 @@ def tile_selfattention_pb_kernel(
                 out=x_raw[h][:, blocks, :], in_=x_view[:, blocks, h * X_POS : (h + 1) * X_POS]
             )
 
-        nc.sync.dma_start(out=q_first[:], in_=q_view[:, 0:Q_TILES, :])
+        nc.sync.dma_start(out=q_first[:], in_=q_view[:, 0, :, :])
         nc.sync.dma_start(out=k_raw[:], in_=k.rearrange("b c n -> (b c) n"))
         nc.sync.dma_start(out=v_raw[:], in_=v.rearrange("b (p j) c -> p (b j) c", j=PACK))
-        nc.sync.dma_start(out=q_rest[:], in_=q_view[:, Q_TILES:TILES, :])
+        nc.sync.dma_start(
+            out=q_rest[:].rearrange("p (part i) c -> p part i c", i=Q_TILES),
+            in_=q_view[:, 1:Q_PARTS, :, :],
+        )
         nc.vector.memset(vec_rows[:], 0.0)
         for j, vec in enumerate((bp, bnp_s, bnp_b, bnp_m, bnp_v)):
             nc.sync.dma_start(
@@ -357,7 +360,12 @@ def tile_selfattention_pb_kernel(
                 else:
                     q_tile = q_rest[:, (part - 1) * Q_TILES + il, :]
                 nc.tensor.transpose(qT_ps[:, il, :], q_tile, ident_bf[:])
-            return lambda: nc.scalar.copy(out=qT[part][:], in_=qT_ps[:])
+            return lambda: nc.scalar.copy(
+                out=qT[part][:].rearrange("c i r -> c (i r)").rearrange(
+                    "c (r i) -> c r i", i=Q_TILES
+                ),
+                in_=qT_ps[:].rearrange("c i r -> c r i"),
+            )
 
         wp_words = wp_raw[:].bitcast(F32).rearrange("r b (p u) -> r b u p", u=2)
         wp_grouped_words = wp_grouped[:].bitcast(F32)

from contextlib import ExitStack

import concourse.mybir as mybir
from concourse.masks import make_identity

F32 = mybir.dt.float32
BF16 = mybir.dt.bfloat16
U32 = mybir.dt.uint32
U8 = mybir.dt.uint8
FP8X4 = mybir.dt.float8_e4m3fn_x4
ALU = mybir.AluOpType
ACT = mybir.ActivationFunctionType
AXIS = mybir.AxisListType

P = 128
PACK = 4
POSITIONS = 2048
QUERY_CH = 128
POOLED = 512
VALUE_CH = 512
OUT_CH = 1024
EPS = 1e-5

TILES = POSITIONS // P
Q_PARTS = 4
Q_TILES = TILES // Q_PARTS
BLOCKS = OUT_CH // P
WP_PARTS = BLOCKS // 2
X_PARTS = 2
X_POS = POSITIONS // X_PARTS
GROUP_TILES = (4, 4, 4, 2, 2)
GROUPS = len(GROUP_TILES)
GROUP_FIRST = [sum(GROUP_TILES[:g]) for g in range(GROUPS)]
GROUP_OF = [g for g in range(GROUPS) for tile in range(GROUP_TILES[g])]
LONG_PLAN = (((0, 1), ()), ((2, 3), ()), ((4, 5), ()), ((6, 7), ()))
SHORT_PLAN = (((0, 1, 2, 3), ()), ((4, 5, 6, 7), ()))
OUTPUT_PLAN = (LONG_PLAN, LONG_PLAN, LONG_PLAN, SHORT_PLAN)
LAST_VECTOR = (0, 1, 2, 3, 4, 5)
LAST_SCALAR = (6, 7)
SHIFTS = tuple((cb, g, g + 4) for g in (0, 4, 8, 12) for cb in range(8))
SHIFTED_BLOCKS = 8

FLOPS = 2 * POSITIONS * POOLED * (QUERY_CH + VALUE_CH) + 2 * OUT_CH * VALUE_CH * POSITIONS


def tile_selfattention_pb_kernel(
    tc, q, k, v, x, wp, bp, bnp_s, bnp_b, bnp_m, bnp_v, gamma, out
):
    nc = tc.nc
    with ExitStack() as ctx:
        ctx.enter_context(tc.manual_schedule())
        const = ctx.enter_context(tc.tile_pool(name="const", bufs=1))
        work = ctx.enter_context(tc.tile_pool(name="work", bufs=3))
        psum = ctx.enter_context(tc.psum_pool(name="psum", bufs=1))

        q_view = q.rearrange("b (part p i) c -> p (b part) i c", p=P, i=Q_TILES)
        x_view = x.rearrange("b (cb p) h w -> p (b cb) (h w)", p=P)
        out_view = out.rearrange("b (cb p) h w -> p (b cb) (h w)", p=P)

        q_first = const.tile([P, Q_TILES, QUERY_CH], BF16)
        q_rest = const.tile([P, TILES - Q_TILES, QUERY_CH], BF16)
        x_raw = []
        for h in range(X_PARTS):
            x_raw.append(const.tile([P, BLOCKS, X_POS], BF16, name="x_raw%d" % h))
        x_shifted = const.tile([P, SHIFTED_BLOCKS, POSITIONS], F32)
        k_raw = const.tile([P, POOLED], BF16)
        v_raw = const.tile([P, PACK, VALUE_CH], BF16)
        wp_raw = const.tile([P, BLOCKS, VALUE_CH], BF16)
        vec_rows = const.tile([P, P], BF16)
        gamma_bf = const.tile([P, 1], BF16)

        def load_x(h, blocks):
            nc.sync.dma_start(
                out=x_raw[h][:, blocks, :], in_=x_view[:, blocks, h * X_POS : (h + 1) * X_POS]
            )

        nc.sync.dma_start(out=q_first[:], in_=q_view[:, 0, :, :])
        nc.sync.dma_start(out=k_raw[:], in_=k.rearrange("b c n -> (b c) n"))
        nc.sync.dma_start(out=v_raw[:], in_=v.rearrange("b (p j) c -> p (b j) c", j=PACK))
        nc.sync.dma_start(
            out=q_rest[:].rearrange("p (part i) c -> p part i c", i=Q_TILES),
            in_=q_view[:, 1:Q_PARTS, :, :],
        )
        nc.vector.memset(vec_rows[:], 0.0)
        for j, vec in enumerate((bp, bnp_s, bnp_b, bnp_m, bnp_v)):
            nc.sync.dma_start(
                out=vec_rows[j * BLOCKS : (j + 1) * BLOCKS, :],
                in_=vec.rearrange("(cb p) -> cb p", p=P),
            )
        nc.sync.dma_start(out=gamma_bf[:], in_=gamma.partition_broadcast(P))
        nc.sync.dma_start(out=wp_raw[:], in_=wp.rearrange("(cb p) c -> p cb c", p=P))
        for h in range(X_PARTS):
            load_x(h, slice(0, 3))
            load_x(h, slice(3, BLOCKS))

        ident_bf = const.tile([P, P], BF16)
        make_identity(nc, ident_bf[:])
        ident_f32 = const.tile([P, P], F32)
        make_identity(nc, ident_f32[:])
        neg_half = const.tile([P, BLOCKS], F32)
        nc.gpsimd.memset(neg_half[:], -0.5)

        warm_in = const.tile([P, 1], F32)
        warm_out = const.tile([P, 1], F32)
        nc.vector.memset(warm_in[:], 0.0)
        nc.scalar.activation(out=warm_out[:], in_=warm_in[:], func=ACT.Exp)

        k_perm = const.tile([P, 2, P, 2], BF16)
        nc.vector.tensor_copy(
            out=k_perm[:], in_=k_raw[:].rearrange("c (p u two) -> c u p two", u=2, two=2)
        )

        neg_max = const.tile([P, TILES], F32)
        row_sum = const.tile([P, TILES], F32)
        inv_sum = const.tile([P, TILES], F32)

        qT = []
        for part in range(Q_PARTS):
            qT.append(const.tile([P, Q_TILES, P], BF16, name="qT%d" % part))

        v_grouped = const.tile([P, VALUE_CH, PACK], BF16, align_bytes=64)
        v_codes = const.tile([P, VALUE_CH], U32, align_bytes=64)
        v_scales = const.tile([P, VALUE_CH], U8, align_bytes=64)
        wp_grouped = const.tile([P, OUT_CH, PACK], BF16, align_bytes=64)
        wp_codes = const.tile([P, OUT_CH], U32, align_bytes=64)
        wp_scales = const.tile([P, OUT_CH], U8, align_bytes=64)

        vec_cols = const.tile([P, 5 * BLOCKS], F32)
        gamma_f32 = const.tile([P, 1], F32)
        var_eps = const.tile([P, BLOCKS], F32)
        rstd = const.tile([P, BLOCKS], F32)
        inv = const.tile([P, BLOCKS], F32)
        centred = const.tile([P, BLOCKS], F32)
        scaled = const.tile([P, BLOCKS], F32)
        shifted = const.tile([P, BLOCKS], F32)
        gain = const.tile([P, BLOCKS], F32)
        shift = const.tile([P, BLOCKS], F32)

        nc.gpsimd.tensor_scalar(
            out=v_grouped[:].rearrange("p (t m) j -> p t m j", t=PACK),
            in0=v_raw[:].rearrange("p j (m t) -> p t m j", t=PACK),
            scalar1=1.0,
            scalar2=0.0,
            op0=ALU.mult,
            op1=ALU.add,
        )

        g_codes = const.tile([P, POSITIONS], U32, align_bytes=64)
        g_scales = const.tile([P, POSITIONS], U8, align_bytes=64)

        def slot(i, count=1):
            return slice(i * P, (i + count) * P)

        s_ps = {}
        e_bf = {}
        eT_ps = {}
        e_grouped = {}
        e_codes = {}
        e_scales = {}
        r_ps = {}
        r_sb = {}
        g_ps = {}
        g_grouped = {}
        y_ps = {}
        o_scalar = {}
        waiting = []

        def scores(i):
            part, il = divmod(i, Q_TILES)
            s_ps[i] = psum.tile([P, POOLED], F32, tag="s", bufs=2, name="s_ps")
            nc.tensor.matmul(
                s_ps[i][:],
                lhsT=qT[part][:, il, :],
                rhs=k_perm[:].rearrange("c u p two -> c (u p two)"),
                start=True,
                stop=True,
            )

        def row_maximum(i):
            nc.vector.tensor_reduce(
                out=neg_max[:, i : i + 1], in_=s_ps[i][:], axis=AXIS.X, op=ALU.max, negate=True
            )

        def exponentials(i):
            e_bf[i] = work.tile([P, POOLED], BF16, tag="e_bf", name="e_bf")
            nc.scalar.activation(
                out=e_bf[i][:],
                in_=s_ps[i][:],
                func=ACT.Exp,
                bias=neg_max[:, i : i + 1],
                scale=1.0,
                accum_out=row_sum[:, i : i + 1],
            )

        def reciprocal_of_sum(i):
            nc.vector.reciprocal(out=inv_sum[:, i : i + 1], in_=row_sum[:, i : i + 1])

        def transpose_e(i):
            eT_ps[i] = psum.tile([P, 2, P], F32, tag="tp", name="eT_ps")
            e_words = e_bf[i][:].bitcast(F32)
            for u in range(2):
                nc.tensor.transpose(
                    eT_ps[i][:, u, :], e_words[:, u * P : (u + 1) * P], ident_f32[:]
                )

        def copy_e(i):
            e_grouped[i] = work.tile(
                [P, P, PACK], BF16, tag="e_grouped", name="e_grouped", align_bytes=64
            )
            nc.scalar.copy(
                out=e_grouped[i][:].bitcast(F32), in_=eT_ps[i][:].rearrange("p u r -> p r u")
            )

        def spread_reciprocals(i):
            r_ps[i] = psum.tile([P, P], F32, tag="r", name="r_ps")
            nc.tensor.transpose(
                r_ps[i][:], inv_sum[:, i : i + 1].to_broadcast([P, P]), ident_f32[:]
            )

        def copy_reciprocals(i):
            r_sb[i] = work.tile([P, P], F32, tag="r_sb", name="r_sb")
            nc.scalar.copy(out=r_sb[i][:], in_=r_ps[i][:])

        def quantise_e(i):
            e_codes[i] = work.tile([P, P], U32, tag="e_codes", name="e_codes", align_bytes=64)
            e_scales[i] = work.tile([P, P], U8, tag="e_scales", name="e_scales", align_bytes=64)
            nc.vector.quantize_mx(
                out=e_codes[i][:].bitcast(FP8X4),
                scales=e_scales[i][:],
                in_=e_grouped[i][:].rearrange("p r t -> p (r t)"),
            )

        def attend(i):
            g_ps[i] = psum.tile([P, PACK, P], F32, tag="g", bufs=1, name="g_ps")
            for t in range(PACK):
                cols = slice(t * P, (t + 1) * P)
                nc.tensor.matmul_mx(
                    out=g_ps[i][:, t, :],
                    lhsT=v_codes[:, cols].bitcast(FP8X4),
                    lhsT_scale=v_scales[:, cols],
                    rhs=e_codes[i][:].bitcast(FP8X4),
                    rhs_scale=e_scales[i][:],
                    start=True,
                    stop=True,
                )

        def normalise(i):
            g_grouped[i] = work.tile(
                [P, P, PACK], BF16, tag="g_grouped", name="g_grouped", align_bytes=64
            )
            nc.vector.tensor_tensor(
                out=g_grouped[i][:],
                in0=g_ps[i][:].rearrange("p t r -> p r t"),
                in1=r_sb[i][:].unsqueeze(2).to_broadcast([P, P, PACK]),
                op=ALU.mult,
            )

        def quantise_g(i):
            nc.vector.quantize_mx(
                out=g_codes[:, slot(i)].bitcast(FP8X4),
                scales=g_scales[:, slot(i)],
                in_=g_grouped[i][:].rearrange("p r t -> p (r t)"),
            )

        def group_columns(g):
            first = GROUP_FIRST[g] * P
            return slice(first, first + GROUP_TILES[g] * P)

        def x_part(blocks, low, high):
            h = low // X_POS
            return x_raw[h][:, blocks, low - h * X_POS : high - h * X_POS]

        def add_shift_on_gpsimd(cb, first_tile, last_tile):
            low, high = first_tile * P, last_tile * P
            nc.gpsimd.tensor_scalar(
                out=x_shifted[:, cb, low:high],
                in0=x_part(cb, low, high),
                scalar1=1.0,
                scalar2=shift[:, cb : cb + 1],
                op0=ALU.mult,
                op1=ALU.add,
            )

        def add_shift_on_scalar(cb, first_tile, last_tile):
            low, high = first_tile * P, last_tile * P
            nc.scalar.activation(
                out=x_shifted[:, cb, low:high],
                in_=x_part(cb, low, high),
                func=ACT.Identity,
                bias=shift[:, cb : cb + 1],
                scale=1.0,
            )

        def project(g, cb, tag="y", bufs=3):
            cols = slice(cb * P, (cb + 1) * P)
            positions = slot(GROUP_FIRST[g], GROUP_TILES[g])
            y_ps[(g, cb)] = psum.tile(
                [P, GROUP_TILES[g] * P], F32, tag=tag, bufs=bufs, name="y_ps"
            )
            nc.tensor.matmul_mx(
                out=y_ps[(g, cb)][:],
                lhsT=wp_codes[:, cols].bitcast(FP8X4),
                lhsT_scale=wp_scales[:, cols],
                rhs=g_codes[:, positions].bitcast(FP8X4),
                rhs_scale=g_scales[:, positions],
                start=True,
                stop=True,
            )

        def finish_on_vector(g, cb):
            cols = group_columns(g)
            nc.vector.scalar_tensor_tensor(
                out=x_shifted[:, cb, cols],
                in0=y_ps[(g, cb)][:],
                scalar=gain[:, cb : cb + 1],
                in1=x_shifted[:, cb, cols],
                op0=ALU.mult,
                op1=ALU.add,
            )

        def store_vector(g, first, last):
            cols = group_columns(g)
            nc.sync.dma_start(
                out=out_view[:, first:last, cols], in_=x_shifted[:, first:last, cols]
            )

        def scale_on_scalar(g, blocks):
            o_scalar[(g, blocks)] = work.tile(
                [P, len(blocks), GROUP_TILES[g] * P], F32, tag="o_scalar", name="o_scalar", bufs=10
            )
            for j, cb in enumerate(blocks):
                nc.scalar.activation(
                    out=o_scalar[(g, blocks)][:, j, :],
                    in_=y_ps[(g, cb)][:],
                    func=ACT.Identity,
                    bias=shift[:, cb : cb + 1],
                    scale=gain[:, cb : cb + 1],
                )

        def add_x(g, blocks, engine):
            cols = group_columns(g)
            engine.tensor_tensor(
                out=o_scalar[(g, blocks)][:],
                in0=o_scalar[(g, blocks)][:],
                in1=x_part(slice(blocks[0], blocks[-1] + 1), cols.start, cols.stop),
                op=ALU.add,
            )

        def store_scalar(g, blocks):
            nc.sync.dma_start(
                out=out_view[:, blocks[0] : blocks[-1] + 1, group_columns(g)],
                in_=o_scalar[(g, blocks)][:],
            )

        def transpose_q(part, tag):
            qT_ps = psum.tile([P, Q_TILES, P], BF16, tag=tag, bufs=3 if tag == "y" else 1)
            for il in range(Q_TILES):
                if part == 0:
                    q_tile = q_first[:, il, :]
                else:
                    q_tile = q_rest[:, (part - 1) * Q_TILES + il, :]
                nc.tensor.transpose(qT_ps[:, il, :], q_tile, ident_bf[:])
            return lambda: nc.scalar.copy(
                out=qT[part][:].rearrange("c i r -> c (i r)").rearrange(
                    "c (r i) -> c r i", i=Q_TILES
                ),
                in_=qT_ps[:].rearrange("c i r -> c r i"),
            )

        wp_words = wp_raw[:].bitcast(F32).rearrange("r b (p u) -> r b u p", u=2)
        wp_grouped_words = wp_grouped[:].bitcast(F32)

        def transpose_wp(pair):
            wT_ps = psum.tile([P, 2, 2, P], F32, tag="y", bufs=3)
            for c in range(2):
                for u in range(2):
                    nc.tensor.transpose(
                        wT_ps[:, c, u, :], wp_words[:, 2 * pair + c, u, :], ident_f32[:]
                    )
            return lambda: nc.scalar.copy(
                out=wp_grouped_words[:, 2 * pair * P : (2 * pair + 2) * P, :].rearrange(
                    "p (c r) u -> p c r u", c=2
                ),
                in_=wT_ps[:].rearrange("p c u r -> p c r u"),
            )

        def quantise_wp(pair):
            rows = slice(2 * pair * P, (2 * pair + 2) * P)
            nc.vector.quantize_mx(
                out=wp_codes[:, rows].bitcast(FP8X4),
                scales=wp_scales[:, rows],
                in_=wp_grouped[:, rows, :].rearrange("p r t -> p (r t)"),
            )

        def quantise_v():
            nc.vector.quantize_mx(
                out=v_codes[:].bitcast(FP8X4),
                scales=v_scales[:],
                in_=v_grouped[:].rearrange("p c j -> p (c j)"),
            )

        def transpose_vectors():
            vec_ps = psum.tile([P, P], BF16, tag="y", bufs=3)
            nc.tensor.transpose(vec_ps[:], vec_rows[:], ident_bf[:])
            return lambda: channel_constants(vec_ps)

        def channel_constants(vec_ps):
            nc.scalar.copy(out=vec_cols[:], in_=vec_ps[:, 0 : 5 * BLOCKS])
            bias_c = vec_cols[:, 0:BLOCKS]
            gain_c = vec_cols[:, BLOCKS : 2 * BLOCKS]
            beta_c = vec_cols[:, 2 * BLOCKS : 3 * BLOCKS]
            mean_c = vec_cols[:, 3 * BLOCKS : 4 * BLOCKS]
            var_c = vec_cols[:, 4 * BLOCKS : 5 * BLOCKS]
            pool = nc.gpsimd
            pool.tensor_scalar(
                out=var_eps[:], in0=var_c, scalar1=1.0, scalar2=EPS, op0=ALU.mult, op1=ALU.add
            )
            pool.tensor_tensor(out=rstd[:], in0=var_eps[:], in1=neg_half[:], op=ALU.pow)
            pool.tensor_copy(out=gamma_f32[:], in_=gamma_bf[:])
            pool.tensor_tensor(out=centred[:], in0=bias_c, in1=mean_c, op=ALU.subtract)
            pool.tensor_tensor(out=inv[:], in0=gain_c, in1=rstd[:], op=ALU.mult)
            pool.tensor_tensor(out=scaled[:], in0=centred[:], in1=inv[:], op=ALU.mult)
            pool.tensor_tensor(out=shifted[:], in0=scaled[:], in1=beta_c, op=ALU.add)
            pool.tensor_scalar(
                out=shift[:],
                in0=shifted[:],
                scalar1=gamma_f32[:, 0:1],
                scalar2=0.0,
                op0=ALU.mult,
                op1=ALU.add,
            )
            pool.tensor_scalar(
                out=gain[:],
                in0=inv[:],
                scalar1=gamma_f32[:, 0:1],
                scalar2=0.0,
                op0=ALU.mult,
                op1=ALU.add,
            )

        LAG = 3

        def tile_in_range(i):
            return 0 <= i < TILES

        vector_work = {}
        scalar_work = {}
        for g in range(len(OUTPUT_PLAN)):
            for s in range(len(OUTPUT_PLAN[g])):
                step = GROUP_FIRST[g] + GROUP_TILES[g] + LAG + s
                vector_blocks, scalar_blocks = OUTPUT_PLAN[g][s]
                vector_work.setdefault(step, []).extend((g, cb) for cb in vector_blocks)
                scalar_work.setdefault(step, []).append((g, scalar_blocks))
        GPSIMD_BY_STEP = {}
        for j, item in enumerate(SHIFTS[:10]):
            GPSIMD_BY_STEP.setdefault(2 + j // 2, []).append(item)
        SCALAR_BY_STEP = {}
        for j, item in enumerate(SHIFTS[10:]):
            SCALAR_BY_STEP.setdefault(6 + j * 11 // 22, []).append(item)
        WP_TRANS = 2
        WP_QUANT = 4
        to_store = []

        transpose_q(0, "tp")()
        scores(0)
        for n in range(TILES + LAG):
            on_vector = vector_work.get(n, [])
            on_scalar = [item for item in scalar_work.get(n, []) if item[1]]
            if tile_in_range(n + 1):
                scores(n + 1)
            if tile_in_range(n):
                row_maximum(n)
            if tile_in_range(n - 1):
                reciprocal_of_sum(n - 1)
            if tile_in_range(n - 3):
                normalise(n - 3)
            if n == 1:
                quantise_v()
            if 0 <= n - WP_QUANT < WP_PARTS:
                quantise_wp(n - WP_QUANT)
            if tile_in_range(n - 2):
                quantise_e(n - 2)
            for g, cb in on_vector[:1] + [(g, blocks[0]) for g, blocks in on_scalar[:1]]:
                project(g, cb)
            if tile_in_range(n - 2):
                spread_reciprocals(n - 2)
            if tile_in_range(n - 1):
                transpose_e(n - 1)
            for g, cb in on_vector:
                if (g, cb) not in y_ps:
                    project(g, cb)
                finish_on_vector(g, cb)
            for g in sorted({g for g, cb in on_vector}):
                mine = [cb for h, cb in on_vector if h == g]
                store_vector(g, mine[0], mine[-1] + 1)
            if tile_in_range(n):
                exponentials(n)
            if tile_in_range(n - 2):
                copy_reciprocals(n - 2)
            if tile_in_range(n - 3):
                quantise_g(n - 3)
            for copy_out in waiting:
                copy_out()
            waiting = []
            if tile_in_range(n - 1):
                copy_e(n - 1)
            if tile_in_range(n - 2):
                attend(n - 2)
            for g, blocks in to_store:
                store_scalar(g, blocks)
            to_store = on_scalar
            if n in (1, 3, 5):
                waiting.append(transpose_q((n + 1) // 2, "y"))
            if n == 0:
                waiting.append(transpose_vectors())
            if 0 <= n - WP_TRANS < WP_PARTS:
                waiting.append(transpose_wp(n - WP_TRANS))
            for item in GPSIMD_BY_STEP.get(n, ()):
                add_shift_on_gpsimd(*item)
            for item in SCALAR_BY_STEP.get(n, ()):
                add_shift_on_scalar(*item)
            for g, blocks in on_scalar:
                for cb in blocks:
                    if (g, cb) not in y_ps:
                        project(g, cb)
                scale_on_scalar(g, blocks)
                add_x(g, blocks, nc.gpsimd)

        g = GROUPS - 1
        banks = [("y", 3), ("s", 2), ("y", 3), ("s", 2), ("y", 3), ("tp", 1), ("r", 1), ("g", 1)]
        order = []
        for j in range(len(LAST_VECTOR)):
            order.extend(LAST_SCALAR[j : j + 1] + LAST_VECTOR[j : j + 1])
        for cb, (tag, bufs) in zip(order, banks):
            project(g, cb, tag, bufs)
        for cb in LAST_SCALAR:
            scale_on_scalar(g, (cb,))
        for cb in LAST_SCALAR[:-1]:
            add_x(g, (cb,), nc.gpsimd)
        for cb in LAST_VECTOR:
            finish_on_vector(g, cb)
        store_vector(g, 0, 3)
        store_vector(g, 3, 6)
        add_x(g, LAST_SCALAR[-1:], nc.vector)
        for cb in LAST_SCALAR[-1:] + LAST_SCALAR[:-1]:
            store_scalar(g, (cb,))
